import numpy as np
import ml_dtypes


def mxq(x, axis, fmt="e4m3"):
    dtype, down = {"e4m3": (ml_dtypes.float8_e4m3fn, 7), "e5m2": (ml_dtypes.float8_e5m2, 14)}[fmt]
    v = np.moveaxis(np.asarray(x, np.float32).astype(ml_dtypes.bfloat16).astype(np.float64), axis, -1)
    blocks = v.reshape(v.shape[:-1] + (-1, 32))
    amax = np.abs(blocks).max(-1, keepdims=True)
    byte = np.maximum(np.where(amax > 0, np.frexp(amax)[1] - 1 + 127, 0) - down, 1)
    scale = np.exp2(byte - 127.0)
    codes = (blocks / scale).astype(np.float32).astype(dtype).astype(np.float64)
    return np.moveaxis((codes * scale).reshape(v.shape), -1, axis)


WIDE = False


def mx_kscale(k):
    if not WIDE:
        return np.ones(k)
    levels = np.array([10, -10, 5, -5, 0])
    if k % 512:
        return np.exp2(np.random.permutation(np.resize(levels, k // 32))).repeat(32)
    a = np.empty((k // 512, 16))
    for p in range(k // 512):
        a[p, :8] = np.random.permutation(np.resize(levels, 8))
        for g in range(8):
            far = levels[np.abs(levels - a[p, g]) >= 10]
            a[p, g + 8] = far[np.random.randint(len(far))]
    return np.exp2(a.ravel()).repeat(32)


BF16 = ml_dtypes.bfloat16


def bf(x):
    return np.asarray(x, np.float32).astype(BF16)


def f64(x):
    return np.asarray(x).astype(np.float64)


B, H, S, D, P = 2, 4, 512, 256, 3


def setup_inputs():
    s = mx_kscale(S)
    g = np.exp2(np.round(np.log2(np.mean(s))))
    sign = np.where(np.random.standard_normal((H, 1)) < 0.0, -1.0, 1.0)
    q = np.random.standard_normal((B, H, S, D)) * 1.5
    k = np.random.standard_normal((B, H, S, D))
    v = np.random.standard_normal((B, H, S, D)) * 2.0
    q[..., 0] = 1.0
    k[..., 0] += np.log(s) * np.sqrt(D)
    v = v / s[:, None] * g
    return {
        "q": bf(q),
        "k": bf(k),
        "v": bf(v),
        "qs_s": bf(np.random.uniform(0.0, 1.0, (B, S, P))),
        "ks_s": bf(np.random.uniform(0.0, 1.0, (B, S, P))),
        "alpha": bf(sign * (1.5 + np.random.uniform(0.0, 1.0, (H, 1)))),
        "beta": bf(1.5 + 0.5 * np.random.standard_normal((H, 1))),
    }


def reference(q, k, v, qs_s, ks_s, alpha, beta):
    scale = 1.0 / np.sqrt(D)
    scores = (f64(q) @ f64(k).transpose(0, 1, 3, 2)) * scale
    d_sq = np.sum(np.square(f64(qs_s)[:, :, None, :] - f64(ks_s)[:, None, :, :]), axis=-1)
    a = f64(alpha)[:, 0][None, :, None, None]
    bexp = f64(beta)[:, 0][None, :, None, None]
    bias = a * np.exp(-bexp * d_sq[:, None, :, :])
    z = scores + bias
    e = np.exp(z - z.max(-1, keepdims=True))
    return (mxq(e, 3, "e4m3") @ mxq(f64(v), 2, "e4m3")) / e.sum(-1, keepdims=True)

@@ -1,0 +1,340 @@
+import math
+from contextlib import ExitStack
+
+import concourse.mybir as mybir
+from concourse.masks import make_identity
+
+F32 = mybir.dt.float32
+BF16 = mybir.dt.bfloat16
+U32 = mybir.dt.uint32
+U8 = mybir.dt.uint8
+FP8X4 = mybir.dt.float8_e4m3fn_x4
+ALU = mybir.AluOpType
+FUNC = mybir.ActivationFunctionType
+AXIS = mybir.AxisListType
+
+B, H, S, D, F = 2, 4, 512, 256, 3
+P = 128
+TILES = S // P
+CHUNKS = D // P
+PACK = 4
+HALVES = 2
+PAIR = 2
+GROUPS = B * TILES
+UNITS = GROUPS * H
+SIDES = 2
+POS_PAD = 32
+
+FLOPS = 2 * 2 * B * H * S * S * D
+
+
+def due(step, first, count):
+    n, rest = divmod(step - first, H)
+    return n if rest == 0 and 0 <= n < count else None
+
+
+def tile_rbfbias_t_kernel(tc, q, k, v, qs_s, ks_s, alpha, beta, out):
+    nc = tc.nc
+    with ExitStack() as ctx:
+        ctx.enter_context(tc.manual_schedule())
+        const = ctx.enter_context(tc.tile_pool(name="const", bufs=1))
+        raw = ctx.enter_context(tc.tile_pool(name="raw", bufs=1))
+        operand = ctx.enter_context(tc.tile_pool(name="operand", bufs=1))
+        work = ctx.enter_context(tc.tile_pool(name="work", bufs=2))
+        psum = ctx.enter_context(tc.psum_pool(name="psum", bufs=2))
+
+        def k_due(step):
+            h, rest = divmod(step + 11, 2)
+            if rest == 0 and 0 <= h < H:
+                return (0, h)
+            h = due(step, 0, H)
+            return None if h is None else (1, h)
+
+        def v_due(step):
+            if 0 <= step + 3 < H:
+                return (0, step + 3)
+            h = due(step, 8, H)
+            return None if h is None else (1, h)
+
+        first_step, last_step = -12, UNITS + 8
+
+        ident_bf = const.tile([P, P], BF16)
+        make_identity(nc, ident_bf[:])
+        ident_f32 = const.tile([P, P], F32)
+        make_identity(nc, ident_f32[:])
+
+        pos = const.tile([P, SIDES, POS_PAD], BF16)
+        nc.scalar.dma_start(
+            out=pos[:, 0, 0 : B * TILES * F].rearrange("p (b x) -> p b x", b=B),
+            in_=qs_s.rearrange("b (p t) f -> p b (t f)", t=TILES),
+        )
+        nc.scalar.dma_start(
+            out=pos[:, 1, 0 : B * TILES * F].rearrange("p (x f) -> p x f", f=F),
+            in_=ks_s.rearrange("b (t p) f -> p (b t) f", p=P),
+        )
+        alpha_bf = const.tile([P, H], BF16)
+        nc.scalar.dma_start(out=alpha_bf[:], in_=alpha.rearrange("h o -> (h o)").partition_broadcast(P))
+        beta_bf = const.tile([P, H], BF16)
+        nc.scalar.dma_start(out=beta_bf[:], in_=beta.rearrange("h o -> (h o)").partition_broadcast(P))
+
+        k_raw, q_raw, v_raw, v_grouped = {}, {}, {}, {}
+        for s in range(first_step, last_step + 1):
+            head = k_due(s)
+            if head is not None:
+                k_raw[head] = raw.tile([P, TILES, D], BF16, name="k_raw_%d_%d" % head)
+                nc.sync.dma_start(out=k_raw[head][:], in_=k[head[0], head[1]].rearrange("(t p) d -> p t d", p=P))
+            g = due(s, -12, GROUPS)
+            if g is not None:
+                q_raw[g] = raw.tile([P, H, D], BF16, name="q_raw_%d" % g)
+                nc.sync.dma_start(
+                    out=q_raw[g][:], in_=q[g // TILES].rearrange("h (p t) d -> t p h d", t=TILES)[g % TILES]
+                )
+            head = v_due(s)
+            if head is not None:
+                v_raw[head] = raw.tile([P, PACK, D], BF16, name="v_raw_%d_%d" % head)
+                nc.sync.dma_start(out=v_raw[head][:], in_=v[head[0], head[1]].rearrange("(p r) d -> p r d", r=PACK))
+                v_grouped[head] = operand.tile([P, D, PACK], BF16, name="v_grouped_%d_%d" % head, align_bytes=64)
+                nc.gpsimd.tensor_scalar(
+                    out=v_grouped[head][:],
+                    in0=v_raw[head][:].rearrange("p r d -> p d r"),
+                    scalar1=1.0,
+                    scalar2=0.0,
+                    op0=ALU.mult,
+                    op1=ALU.add,
+                )
+
+        square_at = (F, 3 * F)
+        ones_at = (3 * F, F)
+        feat = const.tile([P, SIDES, B * TILES, P], BF16)
+        nc.vector.memset(feat[:], 0.0)
+        for side in range(SIDES):
+            nc.vector.memset(feat[:, side, :, ones_at[side] : ones_at[side] + 2 * F], 1.0)
+        x = pos[:, :, 0 : B * TILES * F]
+        half_square = const.tile([P, SIDES, B * TILES * F], F32)
+        nc.vector.scalar_tensor_tensor(out=half_square[:], in0=x, scalar=-0.5, in1=x, op0=ALU.mult, op1=ALU.mult)
+        nc.vector.tensor_copy(out=feat[:, :, :, 0:F], in_=x.rearrange("p s (x f) -> p s x f", f=F))
+        for part in range(2):
+            for side in range(SIDES):
+                exact = half_square[:, side, :].rearrange("p (x f) -> p x f", f=F)
+                hi = feat[:, side, :, square_at[side] : square_at[side] + F]
+                if part == 0:
+                    nc.vector.tensor_copy(out=hi, in_=exact)
+                else:
+                    lo = feat[:, side, :, square_at[side] + F : square_at[side] + 2 * F]
+                    nc.vector.tensor_sub(out=lo, in0=exact, in1=hi)
+        two_beta = const.tile([P, H], F32)
+        nc.vector.tensor_scalar_mul(out=two_beta[:], in0=beta_bf[:], scalar1=2.0)
+        alpha_f32 = const.tile([P, H], F32)
+        nc.vector.tensor_copy(out=alpha_f32[:], in_=alpha_bf[:])
+
+        k_ps, k_t, q_ps, q_t, v_codes, v_scales = {}, {}, {}, {}, {}, {}
+        d_sq, scores, rbf, z, neg_max, row_sum, inv_sum, e_bf = {}, {}, {}, {}, {}, {}, {}, {}
+        e_ps, e_grouped, e_codes, e_scales, acc = {}, {}, {}, {}, {}
+        feat_ps, feat_t = {}, {}
+
+        def turn_features(b):
+            feat_ps[b] = psum.tile([P, SIDES, TILES, P], BF16, tag="acc", name="feat_ps")
+            for side in range(SIDES):
+                for t in range(TILES):
+                    nc.tensor.transpose(feat_ps[b][:, side, t, :], feat[:, side, b * TILES + t, :], ident_bf[:])
+
+        def copy_features(b):
+            feat_t[b] = const.tile([P, SIDES, S], BF16, name="feat_t_%d" % b)
+            nc.vector.tensor_copy(out=feat_t[b][:].rearrange("f s (t p) -> f s t p", p=P), in_=feat_ps[b][:])
+
+        def turn_k(b, h):
+            k_ps[b, h] = psum.tile([P, CHUNKS, S], BF16, tag="turn", name="k_ps")
+            for t in range(TILES):
+                for c in range(CHUNKS):
+                    nc.tensor.transpose(
+                        k_ps[b, h][:, c, t * P : (t + 1) * P], k_raw[b, h][:, t, c * P : (c + 1) * P], ident_bf[:]
+                    )
+
+        def copy_k(b, h):
+            k_t[b, h] = operand.tile([P, CHUNKS, S], BF16, name="k_t_%d_%d" % (b, h))
+            nc.scalar.copy(out=k_t[b, h][:], in_=k_ps[b, h][:])
+
+        def turn_q(g):
+            q_ps[g] = psum.tile([P, H, CHUNKS, P], BF16, tag="turn", name="q_ps")
+            for h in range(H):
+                for c in range(CHUNKS):
+                    nc.tensor.transpose(q_ps[g][:, h, c, :], q_raw[g][:, h, c * P : (c + 1) * P], ident_bf[:])
+
+        def copy_q(g):
+            q_t[g] = work.tile([P, H, CHUNKS, P], BF16, name="q_t", bufs=4)
+            nc.vector.tensor_scalar_mul(out=q_t[g][:], in0=q_ps[g][:], scalar1=1.0 / math.sqrt(D))
+
+        def quantise_v(b, h):
+            v_codes[b, h] = operand.tile([P, D], U32, name="v_codes_%d_%d" % (b, h), align_bytes=64)
+            v_scales[b, h] = operand.tile([P, D], U8, name="v_scales_%d_%d" % (b, h), align_bytes=64)
+            nc.vector.quantize_mx(
+                out=v_codes[b, h][:].bitcast(FP8X4),
+                scales=v_scales[b, h][:],
+                in_=v_grouped[b, h][:].rearrange("p d r -> p (d r)"),
+            )
+
+        def distances(g):
+            b, t = divmod(g, TILES)
+            d_sq[g] = psum.tile([P, S], F32, name="d_sq")
+            nc.tensor.matmul(
+                d_sq[g][:], lhsT=feat_t[b][:, 0, t * P : (t + 1) * P], rhs=feat_t[b][:, 1, :], start=True, stop=True
+            )
+
+        def radial(u):
+            g, h = divmod(u, H)
+            rbf[u] = work.tile([P, S], F32, name="rbf", bufs=6)
+            nc.scalar.activation(out=rbf[u][:], in_=d_sq[g][:], func=FUNC.Exp, scale=two_beta[:, h : h + 1])
+
+        def first_matmul(u):
+            g, h = divmod(u, H)
+            scores[u] = psum.tile([P, S], F32, name="scores")
+            for c in range(CHUNKS):
+                nc.tensor.matmul(
+                    scores[u][:],
+                    lhsT=q_t[g][:, h, c, :],
+                    rhs=k_t[g // TILES, h][:, c, :],
+                    start=(c == 0),
+                    stop=(c == CHUNKS - 1),
+                )
+
+        def logits(u):
+            h = u % H
+            z[u] = work.tile([P, S], F32, name="z", bufs=8)
+            nc.vector.scalar_tensor_tensor(
+                out=z[u][:], in0=rbf[u][:], scalar=alpha_f32[:, h : h + 1], in1=scores[u][:], op0=ALU.mult, op1=ALU.add
+            )
+
+        def row_max(u):
+            g, h = divmod(u, H)
+            if h == 0:
+                neg_max[g] = work.tile([P, H], F32, name="neg_max", bufs=3)
+            nc.vector.tensor_reduce(out=neg_max[g][:, h : h + 1], in_=z[u][:], axis=AXIS.X, op=ALU.max, negate=True)
+
+        def exponent(u):
+            g, h = divmod(u, H)
+            if h == 0:
+                e_bf[g] = work.tile([P, H * S], BF16, name="e_bf", bufs=3)
+                row_sum[g] = work.tile([P, H], F32, name="row_sum", bufs=3)
+            nc.scalar.activation(
+                out=e_bf[g][:, h * S : (h + 1) * S],
+                in_=z[u][:],
+                func=FUNC.Exp,
+                bias=neg_max[g][:, h : h + 1],
+                accum_out=row_sum[g][:, h : h + 1],
+            )
+
+        def turn_e(g, pair):
+            e_words = e_bf[g][:].bitcast(F32)
+            e_ps[g, pair] = psum.tile([P, PAIR, HALVES, P], F32, tag="turn", name="e_ps")
+            for hh in range(PAIR):
+                for u in range(HALVES):
+                    first = (pair * PAIR + hh) * HALVES * P
+                    nc.tensor.transpose(
+                        e_ps[g, pair][:, hh, u, :], e_words[:, first + u : first + HALVES * P : HALVES], ident_f32[:]
+                    )
+
+        def copy_e(g, pair, copy):
+            e_grouped[g, pair] = work.tile([P, PAIR * P * PACK], BF16, name="e_grouped", bufs=4, align_bytes=64)
+            copy(
+                out=e_grouped[g, pair][:].bitcast(F32).rearrange("p (h i u) -> p h i u", h=PAIR, u=HALVES),
+                in_=e_ps[g, pair][:].rearrange("p h u i -> p h i u"),
+            )
+
+        def quantise_e(g, pair):
+            e_codes[g, pair] = work.tile([P, PAIR * P], U32, name="e_codes", bufs=3, align_bytes=64)
+            e_scales[g, pair] = work.tile([P, PAIR * P], U8, name="e_scales", bufs=3, align_bytes=64)
+            nc.vector.quantize_mx(
+                out=e_codes[g, pair][:].bitcast(FP8X4), scales=e_scales[g, pair][:], in_=e_grouped[g, pair][:]
+            )
+
+        def reciprocal(g):
+            inv_sum[g] = work.tile([P, H], F32, name="inv_sum", bufs=3)
+            nc.vector.reciprocal(out=inv_sum[g][:], in_=row_sum[g][:])
+
+        def second_matmul(g, pair):
+            acc[g, pair] = psum.tile([P, PAIR, D], F32, name="acc")
+            for hh in range(PAIR):
+                h = pair * PAIR + hh
+                nc.tensor.matmul_mx(
+                    out=acc[g, pair][:, hh, :],
+                    lhsT=e_codes[g, pair][:, hh * P : (hh + 1) * P].bitcast(FP8X4),
+                    lhsT_scale=e_scales[g, pair][:, hh * P : (hh + 1) * P],
+                    rhs=v_codes[g // TILES, h][:].bitcast(FP8X4),
+                    rhs_scale=v_scales[g // TILES, h][:],
+                    start=True,
+                    stop=True,
+                )
+
+        def normalise(g, pair):
+            b, t = divmod(g, TILES)
+            result = work.tile([P, PAIR, D], F32, bufs=3)
+            for hh in range(PAIR):
+                h = pair * PAIR + hh
+                nc.scalar.activation(
+                    out=result[:, hh, :], in_=acc[g, pair][:, hh, :], func=FUNC.Copy, scale=inv_sum[g][:, h : h + 1]
+                )
+            heads = slice(pair * PAIR, (pair + 1) * PAIR)
+            nc.sync.dma_start(out=out[b].rearrange("h (p t) d -> t p h d", t=TILES)[t, :, heads, :], in_=result[:])
+
+        for s in range(first_step, last_step + 1):
+            if 0 <= s + 5 < UNITS:
+                first_matmul(s + 5)
+            for pair in range(H // PAIR):
+                g = due(s, 2 + 4 * pair, GROUPS)
+                if g is not None:
+                    turn_e(g, pair)
+            head = k_due(s)
+            if head is not None:
+                turn_k(head[0], head[1])
+            g = due(s, -12, GROUPS)
+            if g is not None:
+                turn_q(g)
+            b = due(s, -10, GROUPS)
+            if b is not None and b % TILES == 0:
+                turn_features(b // TILES)
+            for pair in range(H // PAIR):
+                g = due(s, 9 + 2 * pair, GROUPS)
+                if g is not None:
+                    second_matmul(g, pair)
+            g = due(s, -8, GROUPS)
+            if g is not None:
+                distances(g)
+
+            if 0 <= s + 7 < UNITS:
+                radial(s + 7)
+            if 0 <= s < UNITS:
+                exponent(s)
+            head = k_due(s - 1)
+            if head is not None:
+                copy_k(head[0], head[1])
+            g = due(s, 3, GROUPS)
+            if g is not None:
+                copy_e(g, 0, nc.scalar.copy)
+            for pair in range(H // PAIR):
+                g = due(s, 10 + 2 * pair, GROUPS)
+                if g is not None:
+                    normalise(g, pair)
+
+            if 0 <= s + 4 < UNITS:
+                logits(s + 4)
+            if 0 <= s + 3 < UNITS:
+                row_max(s + 3)
+            b = due(s, -9, GROUPS)
+            if b is not None and b % TILES == 0:
+                copy_features(b // TILES)
+            g = due(s, 6, GROUPS)
+            if g is not None:
+                reciprocal(g)
+            for pair in range(H // PAIR):
+                g = due(s, 6 + 2 * pair, GROUPS)
+                if g is not None:
+                    quantise_e(g, pair)
+            g = due(s, 7, GROUPS)
+            if g is not None:
+                copy_e(g, 1, nc.vector.tensor_copy)
+            g = due(s, -11, GROUPS)
+            if g is not None:
+                copy_q(g)
+            head = v_due(s - 3)
+            if head is not None:
+                quantise_v(head[0], head[1])

@@ -11,7 +11,6 @@ U8 = mybir.dt.uint8
 FP8X4 = mybir.dt.float8_e4m3fn_x4
 ALU = mybir.AluOpType
 FUNC = mybir.ActivationFunctionType
-AXIS = mybir.AxisListType
 
 B, H, S, D, F = 2, 4, 512, 256, 3
 P = 128
@@ -23,6 +22,7 @@ PAIR = 2
 GROUPS = B * TILES
 UNITS = GROUPS * H
 SIDES = 2
+TINY = 1e-30
 POS_PAD = 32
 
 FLOPS = 2 * 2 * B * H * S * S * D
@@ -124,11 +124,27 @@ def tile_rbfbias_t_kernel(tc, q, k, v, qs_s, ks_s, alpha, beta, out):
                     nc.vector.tensor_sub(out=lo, in0=exact, in1=hi)
         two_beta = const.tile([P, H], F32)
         nc.vector.tensor_scalar_mul(out=two_beta[:], in0=beta_bf[:], scalar1=2.0)
-        alpha_f32 = const.tile([P, H], F32)
-        nc.vector.tensor_copy(out=alpha_f32[:], in_=alpha_bf[:])
+
+        not_negative = const.tile([P, H], F32)
+        nc.vector.tensor_scalar(out=not_negative[:], in0=alpha_bf[:], scalar1=0.0, scalar2=None, op0=ALU.is_ge)
+        minus_sign = const.tile([P, H], F32)
+        nc.vector.tensor_scalar(
+            out=minus_sign[:], in0=not_negative[:], scalar1=-2.0, scalar2=1.0, op0=ALU.mult, op1=ALU.add
+        )
+        k_scale = const.tile([P, H], F32)
+        nc.vector.tensor_scalar_mul(out=k_scale[:], in0=minus_sign[:], scalar1=-1.0 / math.sqrt(D))
+        height = const.tile([P, H], F32)
+        nc.vector.tensor_tensor(out=height[:], in0=alpha_bf[:], in1=minus_sign[:], op=ALU.mult)
+        nc.vector.tensor_scalar(
+            out=height[:], in0=height[:], scalar1=-1.0, scalar2=TINY, op0=ALU.mult, op1=ALU.max
+        )
+        log_height = const.tile([P, H], F32)
+        nc.scalar.activation(out=log_height[:], in_=height[:], func=FUNC.Ln)
+        exp_ready = const.tile([P, H], F32)
+        nc.scalar.activation(out=exp_ready[:], in_=height[:], func=FUNC.Exp, scale=0.0)
 
         k_ps, k_t, q_ps, q_t, v_codes, v_scales = {}, {}, {}, {}, {}, {}
-        d_sq, scores, rbf, z, neg_max, row_sum, inv_sum, e_bf = {}, {}, {}, {}, {}, {}, {}, {}
+        d_sq, scores, rbf, minus_z, neg_max, row_sum, inv_sum, e_bf = {}, {}, {}, {}, {}, {}, {}, {}
         e_ps, e_grouped, e_codes, e_scales, acc = {}, {}, {}, {}, {}
         feat_ps, feat_t = {}, {}
 
@@ -152,7 +168,7 @@ def tile_rbfbias_t_kernel(tc, q, k, v, qs_s, ks_s, alpha, beta, out):
 
         def copy_k(b, h):
             k_t[b, h] = operand.tile([P, CHUNKS, S], BF16, name="k_t_%d_%d" % (b, h))
-            nc.scalar.copy(out=k_t[b, h][:], in_=k_ps[b, h][:])
+            nc.vector.tensor_scalar_mul(out=k_t[b, h][:], in0=k_ps[b, h][:], scalar1=k_scale[:, h : h + 1])
 
         def turn_q(g):
             q_ps[g] = psum.tile([P, H, CHUNKS, P], BF16, tag="turn", name="q_ps")
@@ -162,7 +178,7 @@ def tile_rbfbias_t_kernel(tc, q, k, v, qs_s, ks_s, alpha, beta, out):
 
         def copy_q(g):
             q_t[g] = work.tile([P, H, CHUNKS, P], BF16, name="q_t", bufs=4)
-            nc.vector.tensor_scalar_mul(out=q_t[g][:], in0=q_ps[g][:], scalar1=1.0 / math.sqrt(D))
+            nc.scalar.copy(out=q_t[g][:], in_=q_ps[g][:])
 
         def quantise_v(b, h):
             v_codes[b, h] = operand.tile([P, D], U32, name="v_codes_%d_%d" % (b, h), align_bytes=64)
@@ -175,15 +191,26 @@ def tile_rbfbias_t_kernel(tc, q, k, v, qs_s, ks_s, alpha, beta, out):
 
         def distances(g):
             b, t = divmod(g, TILES)
-            d_sq[g] = psum.tile([P, S], F32, name="d_sq")
-            nc.tensor.matmul(
-                d_sq[g][:], lhsT=feat_t[b][:, 0, t * P : (t + 1) * P], rhs=feat_t[b][:, 1, :], start=True, stop=True
-            )
+            d_sq[g] = psum.tile([P, TILES, P], F32, name="d_sq")
+            for c in range(TILES):
+                nc.tensor.matmul(
+                    d_sq[g][:, c, :],
+                    lhsT=feat_t[b][:, 1, c * P : (c + 1) * P],
+                    rhs=feat_t[b][:, 0, t * P : (t + 1) * P],
+                    start=True,
+                    stop=True,
+                )
 
         def radial(u):
             g, h = divmod(u, H)
-            rbf[u] = work.tile([P, S], F32, name="rbf", bufs=6)
-            nc.scalar.activation(out=rbf[u][:], in_=d_sq[g][:], func=FUNC.Exp, scale=two_beta[:, h : h + 1])
+            rbf[u] = work.tile([P, TILES, P], F32, name="rbf", bufs=6)
+            nc.scalar.activation(
+                out=rbf[u][:],
+                in_=d_sq[g][:],
+                func=FUNC.Exp,
+                scale=two_beta[:, h : h + 1],
+                bias=log_height[:, h : h + 1],
+            )
 
         def first_matmul(u):
             g, h = divmod(u, H)
@@ -194,21 +221,32 @@ def tile_rbfbias_t_kernel(tc, q, k, v, qs_s, ks_s, alpha, beta, out):
                     lhsT=q_t[g][:, h, c, :],
                     rhs=k_t[g // TILES, h][:, c, :],
                     start=(c == 0),
-                    stop=(c == CHUNKS - 1),
+                    stop=False,
+                )
+            for c in range(TILES):
+                nc.tensor.matmul(
+                    scores[u][:, c * P : (c + 1) * P],
+                    lhsT=rbf[u][:, c, :],
+                    rhs=ident_f32[:],
+                    is_transpose=True,
+                    start=False,
+                    stop=(c == TILES - 1),
                 )
 
         def logits(u):
-            h = u % H
-            z[u] = work.tile([P, S], F32, name="z", bufs=8)
-            nc.vector.scalar_tensor_tensor(
-                out=z[u][:], in0=rbf[u][:], scalar=alpha_f32[:, h : h + 1], in1=scores[u][:], op0=ALU.mult, op1=ALU.add
-            )
-
-        def row_max(u):
             g, h = divmod(u, H)
             if h == 0:
                 neg_max[g] = work.tile([P, H], F32, name="neg_max", bufs=3)
-            nc.vector.tensor_reduce(out=neg_max[g][:, h : h + 1], in_=z[u][:], axis=AXIS.X, op=ALU.max, negate=True)
+            minus_z[u] = work.tile([P, S], F32, name="minus_z", bufs=8)
+            nc.vector.tensor_scalar(
+                out=minus_z[u][:],
+                in0=scores[u][:],
+                scalar1=minus_sign[:, h : h + 1],
+                scalar2=None,
+                op0=ALU.mult,
+                op1=ALU.min,
+                accum_out=neg_max[g][:, h : h + 1],
+            )
 
         def exponent(u):
             g, h = divmod(u, H)
@@ -216,9 +254,10 @@ def tile_rbfbias_t_kernel(tc, q, k, v, qs_s, ks_s, alpha, beta, out):
                 e_bf[g] = work.tile([P, H * S], BF16, name="e_bf", bufs=3)
                 row_sum[g] = work.tile([P, H], F32, name="row_sum", bufs=3)
             nc.scalar.activation(
-                out=e_bf[g][:, h * S : (h + 1) * S],
-                in_=z[u][:],
+                out=e_bf[g][:, h * S : (h + 1) * S].rearrange("i (u p e) -> i u p e", u=HALVES, e=HALVES),
+                in_=minus_z[u][:].rearrange("i (p u e) -> i u p e", u=HALVES, e=HALVES),
                 func=FUNC.Exp,
+                scale=-1.0,
                 bias=neg_max[g][:, h : h + 1],
                 accum_out=row_sum[g][:, h : h + 1],
             )
@@ -228,14 +267,12 @@ def tile_rbfbias_t_kernel(tc, q, k, v, qs_s, ks_s, alpha, beta, out):
             e_ps[g, pair] = psum.tile([P, PAIR, HALVES, P], F32, tag="turn", name="e_ps")
             for hh in range(PAIR):
                 for u in range(HALVES):
-                    first = (pair * PAIR + hh) * HALVES * P
-                    nc.tensor.transpose(
-                        e_ps[g, pair][:, hh, u, :], e_words[:, first + u : first + HALVES * P : HALVES], ident_f32[:]
-                    )
+                    first = ((pair * PAIR + hh) * HALVES + u) * P
+                    nc.tensor.transpose(e_ps[g, pair][:, hh, u, :], e_words[:, first : first + P], ident_f32[:])
 
-        def copy_e(g, pair, copy):
+        def copy_e(g, pair):
             e_grouped[g, pair] = work.tile([P, PAIR * P * PACK], BF16, name="e_grouped", bufs=4, align_bytes=64)
-            copy(
+            nc.vector.tensor_copy(
                 out=e_grouped[g, pair][:].bitcast(F32).rearrange("p (h i u) -> p h i u", h=PAIR, u=HALVES),
                 in_=e_ps[g, pair][:].rearrange("p h u i -> p h i u"),
             )
@@ -270,9 +307,14 @@ def tile_rbfbias_t_kernel(tc, q, k, v, qs_s, ks_s, alpha, beta, out):
             result = work.tile([P, PAIR, D], F32, bufs=3)
             for hh in range(PAIR):
                 h = pair * PAIR + hh
-                nc.scalar.activation(
-                    out=result[:, hh, :], in_=acc[g, pair][:, hh, :], func=FUNC.Copy, scale=inv_sum[g][:, h : h + 1]
-                )
+                if pair == 0:
+                    nc.scalar.activation(
+                        out=result[:, hh, :], in_=acc[g, pair][:, hh, :], func=FUNC.Copy, scale=inv_sum[g][:, h : h + 1]
+                    )
+                else:
+                    nc.vector.tensor_scalar_mul(
+                        out=result[:, hh, :], in0=acc[g, pair][:, hh, :], scalar1=inv_sum[g][:, h : h + 1]
+                    )
             heads = slice(pair * PAIR, (pair + 1) * PAIR)
             nc.sync.dma_start(out=out[b].rearrange("h (p t) d -> t p h d", t=TILES)[t, :, heads, :], in_=result[:])
 
@@ -304,37 +346,34 @@ def tile_rbfbias_t_kernel(tc, q, k, v, qs_s, ks_s, alpha, beta, out):
                 radial(s + 7)
             if 0 <= s < UNITS:
                 exponent(s)
-            head = k_due(s - 1)
-            if head is not None:
-                copy_k(head[0], head[1])
-            g = due(s, 3, GROUPS)
+            g = due(s, -11, GROUPS)
             if g is not None:
-                copy_e(g, 0, nc.scalar.copy)
-            for pair in range(H // PAIR):
-                g = due(s, 10 + 2 * pair, GROUPS)
-                if g is not None:
-                    normalise(g, pair)
+                copy_q(g)
+            g = due(s, 10, GROUPS)
+            if g is not None:
+                normalise(g, 0)
 
             if 0 <= s + 4 < UNITS:
                 logits(s + 4)
-            if 0 <= s + 3 < UNITS:
-                row_max(s + 3)
             b = due(s, -9, GROUPS)
             if b is not None and b % TILES == 0:
                 copy_features(b // TILES)
+            head = k_due(s - 1)
+            if head is not None:
+                copy_k(head[0], head[1])
             g = due(s, 6, GROUPS)
             if g is not None:
                 reciprocal(g)
             for pair in range(H // PAIR):
+                g = due(s, 3 + 4 * pair, GROUPS)
+                if g is not None:
+                    copy_e(g, pair)
                 g = due(s, 6 + 2 * pair, GROUPS)
                 if g is not None:
                     quantise_e(g, pair)
-            g = due(s, 7, GROUPS)
+            g = due(s, 12, GROUPS)
             if g is not None:
-                copy_e(g, 1, nc.vector.tensor_copy)
-            g = due(s, -11, GROUPS)
-            if g is not None:
-                copy_q(g)
+                normalise(g, 1)
             head = v_due(s - 3)
             if head is not None:
                 quantise_v(head[0], head[1])

@@ -63,26 +63,45 @@ def tile_rbfbias_t_kernel(tc, q, k, v, qs_s, ks_s, alpha, beta, out):
         ident_f32 = const.tile([P, P], F32)
         make_identity(nc, ident_f32[:])
 
-        pos = const.tile([P, SIDES, POS_PAD], BF16)
-        nc.scalar.dma_start(
-            out=pos[:, 0, 0 : B * TILES * F].rearrange("p (b x) -> p b x", b=B),
-            in_=qs_s.rearrange("b (p t) f -> p b (t f)", t=TILES),
-        )
-        nc.scalar.dma_start(
-            out=pos[:, 1, 0 : B * TILES * F].rearrange("p (x f) -> p x f", f=F),
-            in_=ks_s.rearrange("b (t p) f -> p (b t) f", p=P),
-        )
         alpha_bf = const.tile([P, H], BF16)
         nc.scalar.dma_start(out=alpha_bf[:], in_=alpha.rearrange("h o -> (h o)").partition_broadcast(P))
+        pos = const.tile([P, SIDES, POS_PAD], BF16)
+        for side, source in enumerate((qs_s, ks_s)):
+            nc.scalar.dma_start(
+                out=pos[:, side, 0 : B * TILES * F].rearrange("p (b x) -> p b x", b=B),
+                in_=source.rearrange("b (p t) f -> p b (t f)", t=TILES),
+            )
         beta_bf = const.tile([P, H], BF16)
         nc.scalar.dma_start(out=beta_bf[:], in_=beta.rearrange("h o -> (h o)").partition_broadcast(P))
+
+        not_negative = const.tile([P, H], F32)
+        nc.gpsimd.tensor_scalar(out=not_negative[:], in0=alpha_bf[:], scalar1=0.0, scalar2=1.0, op0=ALU.is_ge, op1=ALU.mult)
+        minus_sign = const.tile([P, H], F32)
+        nc.gpsimd.tensor_scalar(
+            out=minus_sign[:], in0=not_negative[:], scalar1=-2.0, scalar2=1.0, op0=ALU.mult, op1=ALU.add
+        )
+        k_scale = const.tile([P, H], F32)
+        nc.gpsimd.tensor_scalar(
+            out=k_scale[:], in0=minus_sign[:], scalar1=-1.0 / math.sqrt(D), scalar2=0.0, op0=ALU.mult, op1=ALU.add
+        )
+        height = const.tile([P, H], F32)
+        nc.gpsimd.tensor_tensor(out=height[:], in0=alpha_bf[:], in1=minus_sign[:], op=ALU.mult)
+        nc.gpsimd.tensor_scalar(
+            out=height[:], in0=height[:], scalar1=-1.0, scalar2=TINY, op0=ALU.mult, op1=ALU.max
+        )
+        log_height = const.tile([P, H], F32)
+        nc.scalar.activation(out=log_height[:], in_=height[:], func=FUNC.Ln)
+        exp_ready = const.tile([P, H], F32)
+        nc.scalar.activation(out=exp_ready[:], in_=height[:], func=FUNC.Exp, scale=0.0)
+        two_beta = const.tile([P, H], F32)
+        nc.gpsimd.tensor_scalar(out=two_beta[:], in0=beta_bf[:], scalar1=2.0, scalar2=0.0, op0=ALU.mult, op1=ALU.add)
 
         k_raw, q_raw, v_raw, v_grouped = {}, {}, {}, {}
         for s in range(first_step, last_step + 1):
             head = k_due(s)
             if head is not None:
                 k_raw[head] = raw.tile([P, TILES, D], BF16, name="k_raw_%d_%d" % head)
-                nc.sync.dma_start(out=k_raw[head][:], in_=k[head[0], head[1]].rearrange("(t p) d -> p t d", p=P))
+                nc.sync.dma_start(out=k_raw[head][:], in_=k[head[0], head[1]].rearrange("(p t) d -> p t d", t=TILES))
             g = due(s, -12, GROUPS)
             if g is not None:
                 q_raw[g] = raw.tile([P, H, D], BF16, name="q_raw_%d" % g)
@@ -122,27 +141,6 @@ def tile_rbfbias_t_kernel(tc, q, k, v, qs_s, ks_s, alpha, beta, out):
                 else:
                     lo = feat[:, side, :, square_at[side] + F : square_at[side] + 2 * F]
                     nc.vector.tensor_sub(out=lo, in0=exact, in1=hi)
-        two_beta = const.tile([P, H], F32)
-        nc.vector.tensor_scalar_mul(out=two_beta[:], in0=beta_bf[:], scalar1=2.0)
-
-        not_negative = const.tile([P, H], F32)
-        nc.vector.tensor_scalar(out=not_negative[:], in0=alpha_bf[:], scalar1=0.0, scalar2=None, op0=ALU.is_ge)
-        minus_sign = const.tile([P, H], F32)
-        nc.vector.tensor_scalar(
-            out=minus_sign[:], in0=not_negative[:], scalar1=-2.0, scalar2=1.0, op0=ALU.mult, op1=ALU.add
-        )
-        k_scale = const.tile([P, H], F32)
-        nc.vector.tensor_scalar_mul(out=k_scale[:], in0=minus_sign[:], scalar1=-1.0 / math.sqrt(D))
-        height = const.tile([P, H], F32)
-        nc.vector.tensor_tensor(out=height[:], in0=alpha_bf[:], in1=minus_sign[:], op=ALU.mult)
-        nc.vector.tensor_scalar(
-            out=height[:], in0=height[:], scalar1=-1.0, scalar2=TINY, op0=ALU.mult, op1=ALU.max
-        )
-        log_height = const.tile([P, H], F32)
-        nc.scalar.activation(out=log_height[:], in_=height[:], func=FUNC.Ln)
-        exp_ready = const.tile([P, H], F32)
-        nc.scalar.activation(out=exp_ready[:], in_=height[:], func=FUNC.Exp, scale=0.0)
-
         k_ps, k_t, q_ps, q_t, v_codes, v_scales = {}, {}, {}, {}, {}, {}
         d_sq, scores, rbf, minus_z, neg_max, row_sum, inv_sum, e_bf = {}, {}, {}, {}, {}, {}, {}, {}
         e_ps, e_grouped, e_codes, e_scales, acc = {}, {}, {}, {}, {}
@@ -159,26 +157,26 @@ def tile_rbfbias_t_kernel(tc, q, k, v, qs_s, ks_s, alpha, beta, out):
             nc.vector.tensor_copy(out=feat_t[b][:].rearrange("f s (t p) -> f s t p", p=P), in_=feat_ps[b][:])
 
         def turn_k(b, h):
-            k_ps[b, h] = psum.tile([P, CHUNKS, S], BF16, tag="turn", name="k_ps")
+            k_ps[b, h] = psum.tile([P, S], F32, tag="turn", name="k_ps")
             for t in range(TILES):
-                for c in range(CHUNKS):
-                    nc.tensor.transpose(
-                        k_ps[b, h][:, c, t * P : (t + 1) * P], k_raw[b, h][:, t, c * P : (c + 1) * P], ident_bf[:]
-                    )
+                nc.tensor.transpose(k_ps[b, h][:, t * P : (t + 1) * P], k_raw[b, h][:, t, :].bitcast(F32), ident_f32[:])
 
         def copy_k(b, h):
-            k_t[b, h] = operand.tile([P, CHUNKS, S], BF16, name="k_t_%d_%d" % (b, h))
-            nc.vector.tensor_scalar_mul(out=k_t[b, h][:], in0=k_ps[b, h][:], scalar1=k_scale[:, h : h + 1])
+            k_t[b, h] = operand.tile([P, S, CHUNKS], BF16, name="k_t_%d_%d" % (b, h))
+            nc.vector.tensor_scalar_mul(
+                out=k_t[b, h][:].rearrange("w j c -> w (j c)"),
+                in0=k_ps[b, h][:].bitcast(BF16),
+                scalar1=k_scale[:, h : h + 1],
+            )
 
         def turn_q(g):
-            q_ps[g] = psum.tile([P, H, CHUNKS, P], BF16, tag="turn", name="q_ps")
+            q_ps[g] = psum.tile([P, H, P], F32, tag="turn", name="q_ps")
             for h in range(H):
-                for c in range(CHUNKS):
-                    nc.tensor.transpose(q_ps[g][:, h, c, :], q_raw[g][:, h, c * P : (c + 1) * P], ident_bf[:])
+                nc.tensor.transpose(q_ps[g][:, h, :], q_raw[g][:, h, :].bitcast(F32), ident_f32[:])
 
         def copy_q(g):
-            q_t[g] = work.tile([P, H, CHUNKS, P], BF16, name="q_t", bufs=4)
-            nc.scalar.copy(out=q_t[g][:], in_=q_ps[g][:])
+            q_t[g] = work.tile([P, H * P * CHUNKS], BF16, name="q_t", bufs=4)
+            nc.scalar.copy(out=q_t[g][:].bitcast(F32), in_=q_ps[g][:].rearrange("w h i -> w (h i)"))
 
         def quantise_v(b, h):
             v_codes[b, h] = operand.tile([P, D], U32, name="v_codes_%d_%d" % (b, h), align_bytes=64)
@@ -215,11 +213,12 @@ def tile_rbfbias_t_kernel(tc, q, k, v, qs_s, ks_s, alpha, beta, out):
         def first_matmul(u):
             g, h = divmod(u, H)
             scores[u] = psum.tile([P, S], F32, name="scores")
+            q_heads = q_t[g][:].rearrange("w (h i c) -> w h i c", h=H, c=CHUNKS)
             for c in range(CHUNKS):
                 nc.tensor.matmul(
                     scores[u][:],
-                    lhsT=q_t[g][:, h, c, :],
-                    rhs=k_t[g // TILES, h][:, c, :],
+                    lhsT=q_heads[:, h, :, c],
+                    rhs=k_t[g // TILES, h][:, :, c],
                     start=(c == 0),
                     stop=False,
                 )
@@ -255,7 +254,7 @@ def tile_rbfbias_t_kernel(tc, q, k, v, qs_s, ks_s, alpha, beta, out):
                 row_sum[g] = work.tile([P, H], F32, name="row_sum", bufs=3)
             nc.scalar.activation(
                 out=e_bf[g][:, h * S : (h + 1) * S].rearrange("i (u p e) -> i u p e", u=HALVES, e=HALVES),
-                in_=minus_z[u][:].rearrange("i (p u e) -> i u p e", u=HALVES, e=HALVES),
+                in_=minus_z[u][:].rearrange("i (u e p) -> i u p e", u=HALVES, e=HALVES),
                 func=FUNC.Exp,
                 scale=-1.0,
                 bias=neg_max[g][:, h : h + 1],
@@ -304,7 +303,7 @@ def tile_rbfbias_t_kernel(tc, q, k, v, qs_s, ks_s, alpha, beta, out):
 
         def normalise(g, pair):
             b, t = divmod(g, TILES)
-            result = work.tile([P, PAIR, D], F32, bufs=3)
+            result = work.tile([P, PAIR, D], F32, bufs=6)
             for hh in range(PAIR):
                 h = pair * PAIR + hh
                 if pair == 0:

@@ -22,15 +22,23 @@ PAIR = 2
 GROUPS = B * TILES
 UNITS = GROUPS * H
 SIDES = 2
-TINY = 1e-30
 POS_PAD = 32
 
 FLOPS = 2 * 2 * B * H * S * S * D
 
 
-def due(step, first, count):
-    n, rest = divmod(step - first, H)
+def due(step, first, every, count):
+    n, rest = divmod(step - first, every)
     return n if rest == 0 and 0 <= n < count else None
+
+
+def piece_of(step):
+    if not 0 <= step < UNITS:
+        return None
+    g, h = divmod(step, H)
+    if step >= UNITS - PAIR:
+        return g, range(h, h + 1)
+    return (g, range(h - 1, h + 1)) if h % PAIR == 1 else None
 
 
 def tile_rbfbias_t_kernel(tc, q, k, v, qs_s, ks_s, alpha, beta, out):
@@ -43,39 +51,54 @@ def tile_rbfbias_t_kernel(tc, q, k, v, qs_s, ks_s, alpha, beta, out):
         work = ctx.enter_context(tc.tile_pool(name="work", bufs=2))
         psum = ctx.enter_context(tc.psum_pool(name="psum", bufs=2))
 
+        first_step, last_step = -12, UNITS + 10
+
         def k_due(step):
-            h, rest = divmod(step + 11, 2)
-            if rest == 0 and 0 <= h < H:
+            h = due(step, -11, 2, H)
+            if h is not None:
                 return (0, h)
-            h = due(step, 0, H)
+            h = due(step, -1, H, H)
             return None if h is None else (1, h)
+
+        def q_due(step):
+            if step == first_step:
+                return 0
+            g = due(step, -7 - H, H, GROUPS)
+            return None if g is None or g == 0 else g
 
         def v_due(step):
-            if 0 <= step + 3 < H:
-                return (0, step + 3)
-            h = due(step, 8, H)
+            h = due(step, -3, 1, H)
+            if h is not None:
+                return (0, h)
+            h = due(step, 8, H, H)
             return None if h is None else (1, h)
-
-        first_step, last_step = -12, UNITS + 8
 
         ident_bf = const.tile([P, P], BF16)
         make_identity(nc, ident_bf[:])
         ident_f32 = const.tile([P, P], F32)
         make_identity(nc, ident_f32[:])
 
-        alpha_bf = const.tile([P, H], BF16)
-        nc.scalar.dma_start(out=alpha_bf[:], in_=alpha.rearrange("h o -> (h o)").partition_broadcast(P))
         pos = const.tile([P, SIDES, POS_PAD], BF16)
-        for side, source in enumerate((qs_s, ks_s)):
-            nc.scalar.dma_start(
+        for side, (queue, source) in enumerate(((nc.sync, qs_s), (nc.scalar, ks_s))):
+            queue.dma_start(
                 out=pos[:, side, 0 : B * TILES * F].rearrange("p (b x) -> p b x", b=B),
                 in_=source.rearrange("b (p t) f -> p b (t f)", t=TILES),
             )
+        alpha_bf = const.tile([P, H], BF16)
+        nc.scalar.dma_start(out=alpha_bf[:], in_=alpha.rearrange("h o -> (h o)").partition_broadcast(P))
         beta_bf = const.tile([P, H], BF16)
         nc.scalar.dma_start(out=beta_bf[:], in_=beta.rearrange("h o -> (h o)").partition_broadcast(P))
 
+        squared = const.tile([P, H], F32)
+        nc.gpsimd.tensor_tensor(out=squared[:], in0=alpha_bf[:], in1=alpha_bf[:], op=ALU.mult)
+        log_squared = const.tile([P, H], F32)
+        nc.scalar.activation(out=log_squared[:], in_=squared[:], func=FUNC.Ln)
+        exp_ready = const.tile([P, H], F32)
+        nc.scalar.activation(out=exp_ready[:], in_=squared[:], func=FUNC.Exp, scale=0.0)
         not_negative = const.tile([P, H], F32)
-        nc.gpsimd.tensor_scalar(out=not_negative[:], in0=alpha_bf[:], scalar1=0.0, scalar2=1.0, op0=ALU.is_ge, op1=ALU.mult)
+        nc.gpsimd.tensor_scalar(
+            out=not_negative[:], in0=alpha_bf[:], scalar1=0.0, scalar2=1.0, op0=ALU.is_ge, op1=ALU.mult
+        )
         minus_sign = const.tile([P, H], F32)
         nc.gpsimd.tensor_scalar(
             out=minus_sign[:], in0=not_negative[:], scalar1=-2.0, scalar2=1.0, op0=ALU.mult, op1=ALU.add
@@ -84,17 +107,14 @@ def tile_rbfbias_t_kernel(tc, q, k, v, qs_s, ks_s, alpha, beta, out):
         nc.gpsimd.tensor_scalar(
             out=k_scale[:], in0=minus_sign[:], scalar1=-1.0 / math.sqrt(D), scalar2=0.0, op0=ALU.mult, op1=ALU.add
         )
-        height = const.tile([P, H], F32)
-        nc.gpsimd.tensor_tensor(out=height[:], in0=alpha_bf[:], in1=minus_sign[:], op=ALU.mult)
-        nc.gpsimd.tensor_scalar(
-            out=height[:], in0=height[:], scalar1=-1.0, scalar2=TINY, op0=ALU.mult, op1=ALU.max
-        )
         log_height = const.tile([P, H], F32)
-        nc.scalar.activation(out=log_height[:], in_=height[:], func=FUNC.Ln)
-        exp_ready = const.tile([P, H], F32)
-        nc.scalar.activation(out=exp_ready[:], in_=height[:], func=FUNC.Exp, scale=0.0)
+        nc.gpsimd.tensor_scalar(
+            out=log_height[:], in0=log_squared[:], scalar1=0.5, scalar2=0.0, op0=ALU.mult, op1=ALU.add
+        )
         two_beta = const.tile([P, H], F32)
-        nc.gpsimd.tensor_scalar(out=two_beta[:], in0=beta_bf[:], scalar1=2.0, scalar2=0.0, op0=ALU.mult, op1=ALU.add)
+        nc.gpsimd.tensor_scalar(
+            out=two_beta[:], in0=beta_bf[:], scalar1=2.0, scalar2=0.0, op0=ALU.mult, op1=ALU.add
+        )
 
         k_raw, q_raw, v_raw, v_grouped = {}, {}, {}, {}
         for s in range(first_step, last_step + 1):
@@ -102,7 +122,7 @@ def tile_rbfbias_t_kernel(tc, q, k, v, qs_s, ks_s, alpha, beta, out):
             if head is not None:
                 k_raw[head] = raw.tile([P, TILES, D], BF16, name="k_raw_%d_%d" % head)
                 nc.sync.dma_start(out=k_raw[head][:], in_=k[head[0], head[1]].rearrange("(p t) d -> p t d", t=TILES))
-            g = due(s, -12, GROUPS)
+            g = q_due(s)
             if g is not None:
                 q_raw[g] = raw.tile([P, H, D], BF16, name="q_raw_%d" % g)
                 nc.sync.dma_start(
@@ -147,7 +167,7 @@ def tile_rbfbias_t_kernel(tc, q, k, v, qs_s, ks_s, alpha, beta, out):
         feat_ps, feat_t = {}, {}
 
         def turn_features(b):
-            feat_ps[b] = psum.tile([P, SIDES, TILES, P], BF16, tag="acc", name="feat_ps")
+            feat_ps[b] = psum.tile([P, SIDES, TILES, P], BF16, tag="acc", bufs=2, name="feat_ps")
             for side in range(SIDES):
                 for t in range(TILES):
                     nc.tensor.transpose(feat_ps[b][:, side, t, :], feat[:, side, b * TILES + t, :], ident_bf[:])
@@ -157,7 +177,7 @@ def tile_rbfbias_t_kernel(tc, q, k, v, qs_s, ks_s, alpha, beta, out):
             nc.vector.tensor_copy(out=feat_t[b][:].rearrange("f s (t p) -> f s t p", p=P), in_=feat_ps[b][:])
 
         def turn_k(b, h):
-            k_ps[b, h] = psum.tile([P, S], F32, tag="turn", name="k_ps")
+            k_ps[b, h] = psum.tile([P, S], F32, tag="turn", bufs=2, name="k_ps")
             for t in range(TILES):
                 nc.tensor.transpose(k_ps[b, h][:, t * P : (t + 1) * P], k_raw[b, h][:, t, :].bitcast(F32), ident_f32[:])
 
@@ -170,7 +190,7 @@ def tile_rbfbias_t_kernel(tc, q, k, v, qs_s, ks_s, alpha, beta, out):
             )
 
         def turn_q(g):
-            q_ps[g] = psum.tile([P, H, P], F32, tag="turn", name="q_ps")
+            q_ps[g] = psum.tile([P, H, P], F32, tag="turn", bufs=2, name="q_ps")
             for h in range(H):
                 nc.tensor.transpose(q_ps[g][:, h, :], q_raw[g][:, h, :].bitcast(F32), ident_f32[:])
 
@@ -189,7 +209,7 @@ def tile_rbfbias_t_kernel(tc, q, k, v, qs_s, ks_s, alpha, beta, out):
 
         def distances(g):
             b, t = divmod(g, TILES)
-            d_sq[g] = psum.tile([P, TILES, P], F32, name="d_sq")
+            d_sq[g] = psum.tile([P, TILES, P], F32, name="d_sq", bufs=2)
             for c in range(TILES):
                 nc.tensor.matmul(
                     d_sq[g][:, c, :],
@@ -201,7 +221,7 @@ def tile_rbfbias_t_kernel(tc, q, k, v, qs_s, ks_s, alpha, beta, out):
 
         def radial(u):
             g, h = divmod(u, H)
-            rbf[u] = work.tile([P, TILES, P], F32, name="rbf", bufs=6)
+            rbf[u] = work.tile([P, TILES, P], F32, name="rbf", bufs=8)
             nc.scalar.activation(
                 out=rbf[u][:],
                 in_=d_sq[g][:],
@@ -212,7 +232,7 @@ def tile_rbfbias_t_kernel(tc, q, k, v, qs_s, ks_s, alpha, beta, out):
 
         def first_matmul(u):
             g, h = divmod(u, H)
-            scores[u] = psum.tile([P, S], F32, name="scores")
+            scores[u] = psum.tile([P, S], F32, name="scores", bufs=2)
             q_heads = q_t[g][:].rearrange("w (h i c) -> w h i c", h=H, c=CHUNKS)
             for c in range(CHUNKS):
                 nc.tensor.matmul(
@@ -261,83 +281,89 @@ def tile_rbfbias_t_kernel(tc, q, k, v, qs_s, ks_s, alpha, beta, out):
                 accum_out=row_sum[g][:, h : h + 1],
             )
 
-        def turn_e(g, pair):
+        def turn_e(g, heads):
             e_words = e_bf[g][:].bitcast(F32)
-            e_ps[g, pair] = psum.tile([P, PAIR, HALVES, P], F32, tag="turn", name="e_ps")
-            for hh in range(PAIR):
+            e_ps[g, heads] = psum.tile([P, PAIR, HALVES, P], F32, tag="turn", bufs=2, name="e_ps")
+            for x, h in enumerate(heads):
                 for u in range(HALVES):
-                    first = ((pair * PAIR + hh) * HALVES + u) * P
-                    nc.tensor.transpose(e_ps[g, pair][:, hh, u, :], e_words[:, first : first + P], ident_f32[:])
+                    first = (h * HALVES + u) * P
+                    nc.tensor.transpose(e_ps[g, heads][:, x, u, :], e_words[:, first : first + P], ident_f32[:])
 
-        def copy_e(g, pair):
-            e_grouped[g, pair] = work.tile([P, PAIR * P * PACK], BF16, name="e_grouped", bufs=4, align_bytes=64)
+        def copy_e(g, heads):
+            e_grouped[g, heads] = work.tile([P, PAIR * P * PACK], BF16, name="e_grouped", bufs=4, align_bytes=64)
             nc.vector.tensor_copy(
-                out=e_grouped[g, pair][:].bitcast(F32).rearrange("p (h i u) -> p h i u", h=PAIR, u=HALVES),
-                in_=e_ps[g, pair][:].rearrange("p h u i -> p h i u"),
+                out=e_grouped[g, heads][:, 0 : len(heads) * P * PACK]
+                .bitcast(F32)
+                .rearrange("p (h i u) -> p h i u", h=len(heads), u=HALVES),
+                in_=e_ps[g, heads][:, 0 : len(heads)].rearrange("p h u i -> p h i u"),
             )
 
-        def quantise_e(g, pair):
-            e_codes[g, pair] = work.tile([P, PAIR * P], U32, name="e_codes", bufs=3, align_bytes=64)
-            e_scales[g, pair] = work.tile([P, PAIR * P], U8, name="e_scales", bufs=3, align_bytes=64)
+        def quantise_e(g, heads):
+            e_codes[g, heads] = work.tile([P, PAIR * P], U32, name="e_codes", bufs=3, align_bytes=64)
+            e_scales[g, heads] = work.tile([P, PAIR * P], U8, name="e_scales", bufs=3, align_bytes=64)
+            used = len(heads) * P
             nc.vector.quantize_mx(
-                out=e_codes[g, pair][:].bitcast(FP8X4), scales=e_scales[g, pair][:], in_=e_grouped[g, pair][:]
+                out=e_codes[g, heads][:, 0:used].bitcast(FP8X4),
+                scales=e_scales[g, heads][:, 0:used],
+                in_=e_grouped[g, heads][:, 0 : used * PACK],
             )
 
         def reciprocal(g):
             inv_sum[g] = work.tile([P, H], F32, name="inv_sum", bufs=3)
             nc.vector.reciprocal(out=inv_sum[g][:], in_=row_sum[g][:])
 
-        def second_matmul(g, pair):
-            acc[g, pair] = psum.tile([P, PAIR, D], F32, name="acc")
-            for hh in range(PAIR):
-                h = pair * PAIR + hh
+        def second_matmul(g, heads):
+            acc[g, heads] = psum.tile([P, PAIR, D], F32, name="acc", bufs=2)
+            for x, h in enumerate(heads):
                 nc.tensor.matmul_mx(
-                    out=acc[g, pair][:, hh, :],
-                    lhsT=e_codes[g, pair][:, hh * P : (hh + 1) * P].bitcast(FP8X4),
-                    lhsT_scale=e_scales[g, pair][:, hh * P : (hh + 1) * P],
+                    out=acc[g, heads][:, x, :],
+                    lhsT=e_codes[g, heads][:, x * P : (x + 1) * P].bitcast(FP8X4),
+                    lhsT_scale=e_scales[g, heads][:, x * P : (x + 1) * P],
                     rhs=v_codes[g // TILES, h][:].bitcast(FP8X4),
                     rhs_scale=v_scales[g // TILES, h][:],
                     start=True,
                     stop=True,
                 )
 
-        def normalise(g, pair):
+        def normalise(g, heads):
             b, t = divmod(g, TILES)
             result = work.tile([P, PAIR, D], F32, bufs=6)
-            for hh in range(PAIR):
-                h = pair * PAIR + hh
-                if pair == 0:
+            inv = inv_sum[g][:, heads[0] : heads[0] + len(heads)]
+            if H - 1 in heads:
+                nc.vector.tensor_mul(
+                    out=result[:, 0 : len(heads), :],
+                    in0=acc[g, heads][:, 0 : len(heads), :],
+                    in1=inv.unsqueeze(2).to_broadcast([P, len(heads), D]),
+                )
+            else:
+                for x in range(len(heads)):
                     nc.scalar.activation(
-                        out=result[:, hh, :], in_=acc[g, pair][:, hh, :], func=FUNC.Copy, scale=inv_sum[g][:, h : h + 1]
+                        out=result[:, x, :], in_=acc[g, heads][:, x, :], func=FUNC.Copy, scale=inv[:, x : x + 1]
                     )
-                else:
-                    nc.vector.tensor_scalar_mul(
-                        out=result[:, hh, :], in0=acc[g, pair][:, hh, :], scalar1=inv_sum[g][:, h : h + 1]
-                    )
-            heads = slice(pair * PAIR, (pair + 1) * PAIR)
-            nc.sync.dma_start(out=out[b].rearrange("h (p t) d -> t p h d", t=TILES)[t, :, heads, :], in_=result[:])
+            nc.sync.dma_start(
+                out=out[b].rearrange("h (p t) d -> t p h d", t=TILES)[t, :, heads[0] : heads[0] + len(heads), :],
+                in_=result[:, 0 : len(heads), :],
+            )
 
         for s in range(first_step, last_step + 1):
             if 0 <= s + 5 < UNITS:
                 first_matmul(s + 5)
-            for pair in range(H // PAIR):
-                g = due(s, 2 + 4 * pair, GROUPS)
-                if g is not None:
-                    turn_e(g, pair)
+            piece = piece_of(s - 3)
+            if piece is not None:
+                turn_e(*piece)
             head = k_due(s)
             if head is not None:
                 turn_k(head[0], head[1])
-            g = due(s, -12, GROUPS)
+            g = q_due(s)
             if g is not None:
                 turn_q(g)
-            b = due(s, -10, GROUPS)
-            if b is not None and b % TILES == 0:
-                turn_features(b // TILES)
-            for pair in range(H // PAIR):
-                g = due(s, 9 + 2 * pair, GROUPS)
-                if g is not None:
-                    second_matmul(g, pair)
-            g = due(s, -8, GROUPS)
+            b = due(s, -10, UNITS // B, B)
+            if b is not None:
+                turn_features(b)
+            piece = piece_of(s - 8)
+            if piece is not None:
+                second_matmul(*piece)
+            g = due(s, -8, H, GROUPS)
             if g is not None:
                 distances(g)
 
@@ -345,34 +371,33 @@ def tile_rbfbias_t_kernel(tc, q, k, v, qs_s, ks_s, alpha, beta, out):
                 radial(s + 7)
             if 0 <= s < UNITS:
                 exponent(s)
-            g = due(s, -11, GROUPS)
+            g = q_due(s - 1)
             if g is not None:
                 copy_q(g)
-            g = due(s, 10, GROUPS)
-            if g is not None:
-                normalise(g, 0)
+            piece = piece_of(s - 9)
+            if piece is not None and H - 1 not in piece[1]:
+                normalise(*piece)
 
             if 0 <= s + 4 < UNITS:
                 logits(s + 4)
-            b = due(s, -9, GROUPS)
-            if b is not None and b % TILES == 0:
-                copy_features(b // TILES)
+            b = due(s, -9, UNITS // B, B)
+            if b is not None:
+                copy_features(b)
             head = k_due(s - 1)
             if head is not None:
                 copy_k(head[0], head[1])
-            g = due(s, 6, GROUPS)
+            g = due(s, 6, H, GROUPS)
             if g is not None:
                 reciprocal(g)
-            for pair in range(H // PAIR):
-                g = due(s, 3 + 4 * pair, GROUPS)
-                if g is not None:
-                    copy_e(g, pair)
-                g = due(s, 6 + 2 * pair, GROUPS)
-                if g is not None:
-                    quantise_e(g, pair)
-            g = due(s, 12, GROUPS)
-            if g is not None:
-                normalise(g, 1)
+            piece = piece_of(s - 4)
+            if piece is not None:
+                copy_e(*piece)
+            piece = piece_of(s - 6)
+            if piece is not None:
+                quantise_e(*piece)
+            piece = piece_of(s - 9)
+            if piece is not None and H - 1 in piece[1]:
+                normalise(*piece)
             head = v_due(s - 3)
             if head is not None:
                 quantise_v(head[0], head[1])

@@ -57,13 +57,13 @@ def tile_rbfbias_t_kernel(tc, q, k, v, qs_s, ks_s, alpha, beta, out):
             h = due(step, -11, 2, H)
             if h is not None:
                 return (0, h)
-            h = due(step, -1, H, H)
+            h = due(step, -4, H, H)
             return None if h is None else (1, h)
 
         def q_due(step):
             if step == first_step:
                 return 0
-            g = due(step, -7 - H, H, GROUPS)
+            g = due(step, -10 - H, H, GROUPS)
             return None if g is None or g == 0 else g
 
         def v_due(step):
@@ -167,7 +167,7 @@ def tile_rbfbias_t_kernel(tc, q, k, v, qs_s, ks_s, alpha, beta, out):
         feat_ps, feat_t = {}, {}
 
         def turn_features(b):
-            feat_ps[b] = psum.tile([P, SIDES, TILES, P], BF16, tag="acc", bufs=2, name="feat_ps")
+            feat_ps[b] = psum.tile([P, SIDES, TILES, P], BF16, tag="acc", name="feat_ps")
             for side in range(SIDES):
                 for t in range(TILES):
                     nc.tensor.transpose(feat_ps[b][:, side, t, :], feat[:, side, b * TILES + t, :], ident_bf[:])
@@ -177,7 +177,7 @@ def tile_rbfbias_t_kernel(tc, q, k, v, qs_s, ks_s, alpha, beta, out):
             nc.vector.tensor_copy(out=feat_t[b][:].rearrange("f s (t p) -> f s t p", p=P), in_=feat_ps[b][:])
 
         def turn_k(b, h):
-            k_ps[b, h] = psum.tile([P, S], F32, tag="turn", bufs=2, name="k_ps")
+            k_ps[b, h] = psum.tile([P, S], F32, tag="turn", name="k_ps")
             for t in range(TILES):
                 nc.tensor.transpose(k_ps[b, h][:, t * P : (t + 1) * P], k_raw[b, h][:, t, :].bitcast(F32), ident_f32[:])
 
@@ -190,7 +190,7 @@ def tile_rbfbias_t_kernel(tc, q, k, v, qs_s, ks_s, alpha, beta, out):
             )
 
         def turn_q(g):
-            q_ps[g] = psum.tile([P, H, P], F32, tag="turn", bufs=2, name="q_ps")
+            q_ps[g] = psum.tile([P, H, P], F32, tag="turn", name="q_ps")
             for h in range(H):
                 nc.tensor.transpose(q_ps[g][:, h, :], q_raw[g][:, h, :].bitcast(F32), ident_f32[:])
 
@@ -209,7 +209,7 @@ def tile_rbfbias_t_kernel(tc, q, k, v, qs_s, ks_s, alpha, beta, out):
 
         def distances(g):
             b, t = divmod(g, TILES)
-            d_sq[g] = psum.tile([P, TILES, P], F32, name="d_sq", bufs=2)
+            d_sq[g] = psum.tile([P, TILES, P], F32, name="d_sq", bufs=1)
             for c in range(TILES):
                 nc.tensor.matmul(
                     d_sq[g][:, c, :],
@@ -221,7 +221,7 @@ def tile_rbfbias_t_kernel(tc, q, k, v, qs_s, ks_s, alpha, beta, out):
 
         def radial(u):
             g, h = divmod(u, H)
-            rbf[u] = work.tile([P, TILES, P], F32, name="rbf", bufs=8)
+            rbf[u] = work.tile([P, TILES, P], F32, name="rbf", bufs=10)
             nc.scalar.activation(
                 out=rbf[u][:],
                 in_=d_sq[g][:],
@@ -232,24 +232,25 @@ def tile_rbfbias_t_kernel(tc, q, k, v, qs_s, ks_s, alpha, beta, out):
 
         def first_matmul(u):
             g, h = divmod(u, H)
-            scores[u] = psum.tile([P, S], F32, name="scores", bufs=2)
             q_heads = q_t[g][:].rearrange("w (h i c) -> w h i c", h=H, c=CHUNKS)
             for c in range(CHUNKS):
                 nc.tensor.matmul(
                     scores[u][:],
                     lhsT=q_heads[:, h, :, c],
                     rhs=k_t[g // TILES, h][:, :, c],
-                    start=(c == 0),
-                    stop=False,
+                    start=(u % 2 == 1 and c == 0),
+                    stop=(u % 2 == 0 and c == CHUNKS - 1),
                 )
+
+        def add_bias(u):
             for c in range(TILES):
                 nc.tensor.matmul(
                     scores[u][:, c * P : (c + 1) * P],
                     lhsT=rbf[u][:, c, :],
                     rhs=ident_f32[:],
                     is_transpose=True,
-                    start=False,
-                    stop=(c == TILES - 1),
+                    start=(u % 2 == 0 and c == 0),
+                    stop=(u % 2 == 1 and c == TILES - 1),
                 )
 
         def logits(u):
@@ -283,7 +284,7 @@ def tile_rbfbias_t_kernel(tc, q, k, v, qs_s, ks_s, alpha, beta, out):
 
         def turn_e(g, heads):
             e_words = e_bf[g][:].bitcast(F32)
-            e_ps[g, heads] = psum.tile([P, PAIR, HALVES, P], F32, tag="turn", bufs=2, name="e_ps")
+            e_ps[g, heads] = psum.tile([P, PAIR, HALVES, P], F32, tag="turn", name="e_ps")
             for x, h in enumerate(heads):
                 for u in range(HALVES):
                     first = (h * HALVES + u) * P
@@ -313,7 +314,7 @@ def tile_rbfbias_t_kernel(tc, q, k, v, qs_s, ks_s, alpha, beta, out):
             nc.vector.reciprocal(out=inv_sum[g][:], in_=row_sum[g][:])
 
         def second_matmul(g, heads):
-            acc[g, heads] = psum.tile([P, PAIR, D], F32, name="acc", bufs=2)
+            acc[g, heads] = psum.tile([P, PAIR, D], F32, name="acc")
             for x, h in enumerate(heads):
                 nc.tensor.matmul_mx(
                     out=acc[g, heads][:, x, :],
@@ -346,8 +347,6 @@ def tile_rbfbias_t_kernel(tc, q, k, v, qs_s, ks_s, alpha, beta, out):
             )
 
         for s in range(first_step, last_step + 1):
-            if 0 <= s + 5 < UNITS:
-                first_matmul(s + 5)
             piece = piece_of(s - 3)
             if piece is not None:
                 turn_e(*piece)
@@ -357,45 +356,57 @@ def tile_rbfbias_t_kernel(tc, q, k, v, qs_s, ks_s, alpha, beta, out):
             g = q_due(s)
             if g is not None:
                 turn_q(g)
-            b = due(s, -10, UNITS // B, B)
+            b = due(s, -12, UNITS // B, B)
             if b is not None:
                 turn_features(b)
-            piece = piece_of(s - 8)
-            if piece is not None:
-                second_matmul(*piece)
-            g = due(s, -8, H, GROUPS)
+            u = s + 6
+            if 0 <= u < UNITS:
+                scores[u] = psum.tile([P, S], F32, name="scores", bufs=3)
+                if u % 2 == 0:
+                    add_bias(u)
+                    first_matmul(u)
+                else:
+                    first_matmul(u)
+                    add_bias(u)
+            g = due(s, -10, H, GROUPS)
             if g is not None:
                 distances(g)
+            piece = piece_of(s - 7)
+            if piece is not None:
+                second_matmul(*piece)
 
-            if 0 <= s + 7 < UNITS:
-                radial(s + 7)
+            g, half = divmod(s + 8, H)
+            if 0 <= g < GROUPS and half < 2:
+                radial(g * H + 2 * half)
             if 0 <= s < UNITS:
                 exponent(s)
+            if 0 <= g < GROUPS and half < 2:
+                radial(g * H + 2 * half + 1)
             g = q_due(s - 1)
             if g is not None:
                 copy_q(g)
-            piece = piece_of(s - 9)
+            piece = piece_of(s - 8)
             if piece is not None and H - 1 not in piece[1]:
                 normalise(*piece)
 
+            piece = piece_of(s - 4)
+            if piece is not None:
+                copy_e(*piece)
             if 0 <= s + 4 < UNITS:
                 logits(s + 4)
-            b = due(s, -9, UNITS // B, B)
+            b = due(s, -11, UNITS // B, B)
             if b is not None:
                 copy_features(b)
             head = k_due(s - 1)
             if head is not None:
                 copy_k(head[0], head[1])
-            g = due(s, 6, H, GROUPS)
+            g = due(s, 5, H, GROUPS)
             if g is not None:
                 reciprocal(g)
-            piece = piece_of(s - 4)
-            if piece is not None:
-                copy_e(*piece)
-            piece = piece_of(s - 6)
+            piece = piece_of(s - 5)
             if piece is not None:
                 quantise_e(*piece)
-            piece = piece_of(s - 9)
+            piece = piece_of(s - 8)
             if piece is not None and H - 1 in piece[1]:
                 normalise(*piece)
             head = v_due(s - 3)

@@ -22,6 +22,9 @@ PAIR = 2
 GROUPS = B * TILES
 UNITS = GROUPS * H
 SIDES = 2
+VECTOR_GROUPS = (0,)
+FEATURE_PARTS = (range(0, TILES + 1), range(TILES + 1, SIDES * TILES))
+BANKS = {"scores": 3, "d_sq": 1, "turn": 2, "acc": 2}
 POS_PAD = 32
 
 FLOPS = 2 * 2 * B * H * S * S * D
@@ -63,7 +66,7 @@ def tile_rbfbias_t_kernel(tc, q, k, v, qs_s, ks_s, alpha, beta, out):
         def q_due(step):
             if step == first_step:
                 return 0
-            g = due(step, -10 - H, H, GROUPS)
+            g = due(step, -6 - H, H, GROUPS)
             return None if g is None or g == 0 else g
 
         def v_due(step):
@@ -166,18 +169,21 @@ def tile_rbfbias_t_kernel(tc, q, k, v, qs_s, ks_s, alpha, beta, out):
         e_ps, e_grouped, e_codes, e_scales, acc = {}, {}, {}, {}, {}
         feat_ps, feat_t = {}, {}
 
-        def turn_features(b):
-            feat_ps[b] = psum.tile([P, SIDES, TILES, P], BF16, tag="acc", name="feat_ps")
-            for side in range(SIDES):
-                for t in range(TILES):
-                    nc.tensor.transpose(feat_ps[b][:, side, t, :], feat[:, side, b * TILES + t, :], ident_bf[:])
+        def turn_features(b, part):
+            slots = FEATURE_PARTS[part]
+            feat_ps[b, part] = psum.tile([P, len(slots), P], BF16, tag="acc", bufs=BANKS["acc"], name="feat_ps")
+            for x, slot in enumerate(slots):
+                side, t = 1 - slot // TILES, slot % TILES
+                nc.tensor.transpose(feat_ps[b, part][:, x, :], feat[:, side, b * TILES + t, :], ident_bf[:])
 
-        def copy_features(b):
-            feat_t[b] = const.tile([P, SIDES, S], BF16, name="feat_t_%d" % b)
-            nc.vector.tensor_copy(out=feat_t[b][:].rearrange("f s (t p) -> f s t p", p=P), in_=feat_ps[b][:])
+        def copy_features(b, part):
+            if part == 0:
+                feat_t[b] = const.tile([P, SIDES * TILES, P], BF16, name="feat_t_%d" % b)
+            slots = FEATURE_PARTS[part]
+            nc.vector.tensor_copy(out=feat_t[b][:, slots[0] : slots[-1] + 1, :], in_=feat_ps[b, part][:])
 
         def turn_k(b, h):
-            k_ps[b, h] = psum.tile([P, S], F32, tag="turn", name="k_ps")
+            k_ps[b, h] = psum.tile([P, S], F32, tag="turn", bufs=BANKS["turn"], name="k_ps")
             for t in range(TILES):
                 nc.tensor.transpose(k_ps[b, h][:, t * P : (t + 1) * P], k_raw[b, h][:, t, :].bitcast(F32), ident_f32[:])
 
@@ -190,7 +196,7 @@ def tile_rbfbias_t_kernel(tc, q, k, v, qs_s, ks_s, alpha, beta, out):
             )
 
         def turn_q(g):
-            q_ps[g] = psum.tile([P, H, P], F32, tag="turn", name="q_ps")
+            q_ps[g] = psum.tile([P, H, P], F32, tag="turn", bufs=BANKS["turn"], name="q_ps")
             for h in range(H):
                 nc.tensor.transpose(q_ps[g][:, h, :], q_raw[g][:, h, :].bitcast(F32), ident_f32[:])
 
@@ -209,19 +215,19 @@ def tile_rbfbias_t_kernel(tc, q, k, v, qs_s, ks_s, alpha, beta, out):
 
         def distances(g):
             b, t = divmod(g, TILES)
-            d_sq[g] = psum.tile([P, TILES, P], F32, name="d_sq", bufs=1)
+            d_sq[g] = psum.tile([P, S], F32, tag="d_sq", bufs=BANKS["d_sq"], name="d_sq")
+            queries = feat_t[b][:, TILES + t, :]
+            keys = feat_t[b][:, 0:TILES, :].rearrange("f t p -> f (t p)")
+            if g in VECTOR_GROUPS:
+                nc.tensor.matmul(d_sq[g][:], lhsT=queries, rhs=keys, start=True, stop=True)
+                return
             for c in range(TILES):
-                nc.tensor.matmul(
-                    d_sq[g][:, c, :],
-                    lhsT=feat_t[b][:, 1, c * P : (c + 1) * P],
-                    rhs=feat_t[b][:, 0, t * P : (t + 1) * P],
-                    start=True,
-                    stop=True,
-                )
+                columns = slice(c * P, (c + 1) * P)
+                nc.tensor.matmul(d_sq[g][:, columns], lhsT=keys[:, columns], rhs=queries, start=True, stop=True)
 
         def radial(u):
             g, h = divmod(u, H)
-            rbf[u] = work.tile([P, TILES, P], F32, name="rbf", bufs=10)
+            rbf[u] = work.tile([P, S], F32, name="rbf", bufs=10)
             nc.scalar.activation(
                 out=rbf[u][:],
                 in_=d_sq[g][:],
@@ -238,15 +244,17 @@ def tile_rbfbias_t_kernel(tc, q, k, v, qs_s, ks_s, alpha, beta, out):
                     scores[u][:],
                     lhsT=q_heads[:, h, :, c],
                     rhs=k_t[g // TILES, h][:, :, c],
-                    start=(u % 2 == 1 and c == 0),
-                    stop=(u % 2 == 0 and c == CHUNKS - 1),
+                    start=(c == 0 and (u % 2 == 1 or g in VECTOR_GROUPS)),
+                    stop=(c == CHUNKS - 1 and (u % 2 == 0 or g in VECTOR_GROUPS)),
                 )
 
         def add_bias(u):
+            if u // H in VECTOR_GROUPS:
+                return
             for c in range(TILES):
                 nc.tensor.matmul(
                     scores[u][:, c * P : (c + 1) * P],
-                    lhsT=rbf[u][:, c, :],
+                    lhsT=rbf[u][:, c * P : (c + 1) * P],
                     rhs=ident_f32[:],
                     is_transpose=True,
                     start=(u % 2 == 0 and c == 0),
@@ -258,9 +266,13 @@ def tile_rbfbias_t_kernel(tc, q, k, v, qs_s, ks_s, alpha, beta, out):
             if h == 0:
                 neg_max[g] = work.tile([P, H], F32, name="neg_max", bufs=3)
             minus_z[u] = work.tile([P, S], F32, name="minus_z", bufs=8)
+            total = scores[u]
+            if g in VECTOR_GROUPS:
+                total = work.tile([P, S], F32, name="total", bufs=3)
+                nc.vector.tensor_add(out=total[:], in0=rbf[u][:], in1=scores[u][:])
             nc.vector.tensor_scalar(
                 out=minus_z[u][:],
-                in0=scores[u][:],
+                in0=total[:],
                 scalar1=minus_sign[:, h : h + 1],
                 scalar2=None,
                 op0=ALU.mult,
@@ -284,15 +296,16 @@ def tile_rbfbias_t_kernel(tc, q, k, v, qs_s, ks_s, alpha, beta, out):
 
         def turn_e(g, heads):
             e_words = e_bf[g][:].bitcast(F32)
-            e_ps[g, heads] = psum.tile([P, PAIR, HALVES, P], F32, tag="turn", name="e_ps")
+            bank = "scores" if g == GROUPS - 1 else "turn"
+            e_ps[g, heads] = psum.tile([P, PAIR, HALVES, P], F32, tag=bank, bufs=BANKS[bank], name="e_ps")
             for x, h in enumerate(heads):
                 for u in range(HALVES):
                     first = (h * HALVES + u) * P
                     nc.tensor.transpose(e_ps[g, heads][:, x, u, :], e_words[:, first : first + P], ident_f32[:])
 
-        def copy_e(g, heads):
+        def copy_e(g, heads, copy):
             e_grouped[g, heads] = work.tile([P, PAIR * P * PACK], BF16, name="e_grouped", bufs=4, align_bytes=64)
-            nc.vector.tensor_copy(
+            copy(
                 out=e_grouped[g, heads][:, 0 : len(heads) * P * PACK]
                 .bitcast(F32)
                 .rearrange("p (h i u) -> p h i u", h=len(heads), u=HALVES),
@@ -314,7 +327,7 @@ def tile_rbfbias_t_kernel(tc, q, k, v, qs_s, ks_s, alpha, beta, out):
             nc.vector.reciprocal(out=inv_sum[g][:], in_=row_sum[g][:])
 
         def second_matmul(g, heads):
-            acc[g, heads] = psum.tile([P, PAIR, D], F32, name="acc")
+            acc[g, heads] = psum.tile([P, PAIR, D], F32, tag="acc", bufs=BANKS["acc"], name="acc")
             for x, h in enumerate(heads):
                 nc.tensor.matmul_mx(
                     out=acc[g, heads][:, x, :],
@@ -347,7 +360,7 @@ def tile_rbfbias_t_kernel(tc, q, k, v, qs_s, ks_s, alpha, beta, out):
             )
 
         for s in range(first_step, last_step + 1):
-            piece = piece_of(s - 3)
+            piece = piece_of(s - 1)
             if piece is not None:
                 turn_e(*piece)
             head = k_due(s)
@@ -356,12 +369,13 @@ def tile_rbfbias_t_kernel(tc, q, k, v, qs_s, ks_s, alpha, beta, out):
             g = q_due(s)
             if g is not None:
                 turn_q(g)
-            b = due(s, -12, UNITS // B, B)
-            if b is not None:
-                turn_features(b)
+            for part in range(2):
+                b = due(s, -12 + 2 * part, UNITS // B, B)
+                if b is not None:
+                    turn_features(b, part)
             u = s + 6
             if 0 <= u < UNITS:
-                scores[u] = psum.tile([P, S], F32, name="scores", bufs=3)
+                scores[u] = psum.tile([P, S], F32, tag="scores", bufs=BANKS["scores"], name="scores")
                 if u % 2 == 0:
                     add_bias(u)
                     first_matmul(u)
@@ -371,42 +385,46 @@ def tile_rbfbias_t_kernel(tc, q, k, v, qs_s, ks_s, alpha, beta, out):
             g = due(s, -10, H, GROUPS)
             if g is not None:
                 distances(g)
-            piece = piece_of(s - 7)
+            piece = piece_of(s - 5)
             if piece is not None:
                 second_matmul(*piece)
 
             g, half = divmod(s + 8, H)
             if 0 <= g < GROUPS and half < 2:
                 radial(g * H + 2 * half)
-            if 0 <= s < UNITS:
-                exponent(s)
+            if 0 <= s + 2 < UNITS:
+                exponent(s + 2)
             if 0 <= g < GROUPS and half < 2:
                 radial(g * H + 2 * half + 1)
             g = q_due(s - 1)
             if g is not None:
                 copy_q(g)
-            piece = piece_of(s - 8)
+            piece = piece_of(s - 2)
+            if piece is not None and piece[0] == GROUPS - 1:
+                copy_e(*piece, nc.scalar.copy)
+            piece = piece_of(s - 6)
             if piece is not None and H - 1 not in piece[1]:
                 normalise(*piece)
 
-            piece = piece_of(s - 4)
-            if piece is not None:
-                copy_e(*piece)
+            piece = piece_of(s - 2)
+            if piece is not None and piece[0] < GROUPS - 1:
+                copy_e(*piece, nc.vector.tensor_copy)
             if 0 <= s + 4 < UNITS:
                 logits(s + 4)
-            b = due(s, -11, UNITS // B, B)
-            if b is not None:
-                copy_features(b)
+            for part in range(2):
+                b = due(s, -11 + 2 * part, UNITS // B, B)
+                if b is not None:
+                    copy_features(b, part)
             head = k_due(s - 1)
             if head is not None:
                 copy_k(head[0], head[1])
-            g = due(s, 5, H, GROUPS)
+            g = due(s, 3, H, GROUPS)
             if g is not None:
                 reciprocal(g)
-            piece = piece_of(s - 5)
+            piece = piece_of(s - 3)
             if piece is not None:
                 quantise_e(*piece)
-            piece = piece_of(s - 8)
+            piece = piece_of(s - 6)
             if piece is not None and H - 1 in piece[1]:
                 normalise(*piece)
             head = v_due(s - 3)

@@ -73,7 +73,7 @@ def tile_rbfbias_t_kernel(tc, q, k, v, qs_s, ks_s, alpha, beta, out):
             h = due(step, -3, 1, H)
             if h is not None:
                 return (0, h)
-            h = due(step, 8, H, H)
+            h = due(step, 4, H, H)
             return None if h is None else (1, h)
 
         ident_bf = const.tile([P, P], BF16)
@@ -98,26 +98,6 @@ def tile_rbfbias_t_kernel(tc, q, k, v, qs_s, ks_s, alpha, beta, out):
         nc.scalar.activation(out=log_squared[:], in_=squared[:], func=FUNC.Ln)
         exp_ready = const.tile([P, H], F32)
         nc.scalar.activation(out=exp_ready[:], in_=squared[:], func=FUNC.Exp, scale=0.0)
-        not_negative = const.tile([P, H], F32)
-        nc.gpsimd.tensor_scalar(
-            out=not_negative[:], in0=alpha_bf[:], scalar1=0.0, scalar2=1.0, op0=ALU.is_ge, op1=ALU.mult
-        )
-        minus_sign = const.tile([P, H], F32)
-        nc.gpsimd.tensor_scalar(
-            out=minus_sign[:], in0=not_negative[:], scalar1=-2.0, scalar2=1.0, op0=ALU.mult, op1=ALU.add
-        )
-        k_scale = const.tile([P, H], F32)
-        nc.gpsimd.tensor_scalar(
-            out=k_scale[:], in0=minus_sign[:], scalar1=-1.0 / math.sqrt(D), scalar2=0.0, op0=ALU.mult, op1=ALU.add
-        )
-        log_height = const.tile([P, H], F32)
-        nc.gpsimd.tensor_scalar(
-            out=log_height[:], in0=log_squared[:], scalar1=0.5, scalar2=0.0, op0=ALU.mult, op1=ALU.add
-        )
-        two_beta = const.tile([P, H], F32)
-        nc.gpsimd.tensor_scalar(
-            out=two_beta[:], in0=beta_bf[:], scalar1=2.0, scalar2=0.0, op0=ALU.mult, op1=ALU.add
-        )
 
         k_raw, q_raw, v_raw, v_grouped = {}, {}, {}, {}
         for s in range(first_step, last_step + 1):
@@ -164,6 +144,20 @@ def tile_rbfbias_t_kernel(tc, q, k, v, qs_s, ks_s, alpha, beta, out):
                 else:
                     lo = feat[:, side, :, square_at[side] + F : square_at[side] + 2 * F]
                     nc.vector.tensor_sub(out=lo, in0=exact, in1=hi)
+
+        not_negative = const.tile([P, H], F32)
+        nc.vector.tensor_scalar(out=not_negative[:], in0=alpha_bf[:], scalar1=0.0, scalar2=None, op0=ALU.is_ge)
+        minus_sign = const.tile([P, H], F32)
+        nc.vector.tensor_scalar(
+            out=minus_sign[:], in0=not_negative[:], scalar1=-2.0, scalar2=1.0, op0=ALU.mult, op1=ALU.add
+        )
+        k_scale = const.tile([P, H], F32)
+        nc.vector.tensor_scalar_mul(out=k_scale[:], in0=minus_sign[:], scalar1=-1.0 / math.sqrt(D))
+        log_height = const.tile([P, H], F32)
+        nc.vector.tensor_scalar_mul(out=log_height[:], in0=log_squared[:], scalar1=0.5)
+        two_beta = const.tile([P, H], F32)
+        nc.vector.tensor_scalar_mul(out=two_beta[:], in0=beta_bf[:], scalar1=2.0)
+
         k_ps, k_t, q_ps, q_t, v_codes, v_scales = {}, {}, {}, {}, {}, {}
         d_sq, scores, rbf, minus_z, neg_max, row_sum, inv_sum, e_bf = {}, {}, {}, {}, {}, {}, {}, {}
         e_ps, e_grouped, e_codes, e_scales, acc = {}, {}, {}, {}, {}
@@ -427,6 +421,6 @@ def tile_rbfbias_t_kernel(tc, q, k, v, qs_s, ks_s, alpha, beta, out):
             piece = piece_of(s - 6)
             if piece is not None and H - 1 in piece[1]:
                 normalise(*piece)
-            head = v_due(s - 3)
+            head = v_due(s - 7)
             if head is not None:
                 quantise_v(head[0], head[1])

@@ -25,6 +25,7 @@ SIDES = 2
 VECTOR_GROUPS = (0,)
 FEATURE_PARTS = (range(0, TILES + 1), range(TILES + 1, SIDES * TILES))
 BANKS = {"scores": 3, "d_sq": 1, "turn": 2, "acc": 2}
+KEEP_WARM = {-12: 2, -11: 1, -10: 1}
 POS_PAD = 32
 
 FLOPS = 2 * 2 * B * H * S * S * D
@@ -76,6 +77,8 @@ def tile_rbfbias_t_kernel(tc, q, k, v, qs_s, ks_s, alpha, beta, out):
             h = due(step, 4, H, H)
             return None if h is None else (1, h)
 
+        zeros = const.tile([P, S], BF16)
+        nc.gpsimd.memset(zeros[:], 0.0)
         ident_bf = const.tile([P, P], BF16)
         make_identity(nc, ident_bf[:])
         ident_f32 = const.tile([P, P], F32)
@@ -207,6 +210,10 @@ def tile_rbfbias_t_kernel(tc, q, k, v, qs_s, ks_s, alpha, beta, out):
                 in_=v_grouped[b, h][:].rearrange("p d r -> p (d r)"),
             )
 
+        def keep_warm():
+            idle = psum.tile([P, S], F32, tag="scores", bufs=BANKS["scores"], name="idle")
+            nc.tensor.matmul(idle[:], lhsT=zeros[:, 0:P], rhs=zeros[:], start=True, stop=True)
+
         def distances(g):
             b, t = divmod(g, TILES)
             d_sq[g] = psum.tile([P, S], F32, tag="d_sq", bufs=BANKS["d_sq"], name="d_sq")
@@ -321,7 +328,10 @@ def tile_rbfbias_t_kernel(tc, q, k, v, qs_s, ks_s, alpha, beta, out):
             nc.vector.reciprocal(out=inv_sum[g][:], in_=row_sum[g][:])
 
         def second_matmul(g, heads):
-            acc[g, heads] = psum.tile([P, PAIR, D], F32, tag="acc", bufs=BANKS["acc"], name="acc")
+            bank = "acc"
+            if g == GROUPS - 1:
+                bank = "turn" if H - 1 not in heads else "d_sq"
+            acc[g, heads] = psum.tile([P, PAIR, D], F32, tag=bank, bufs=BANKS[bank], name="acc")
             for x, h in enumerate(heads):
                 nc.tensor.matmul_mx(
                     out=acc[g, heads][:, x, :],
@@ -354,6 +364,8 @@ def tile_rbfbias_t_kernel(tc, q, k, v, qs_s, ks_s, alpha, beta, out):
             )
 
         for s in range(first_step, last_step + 1):
+            for extra in range(KEEP_WARM.get(s, 0)):
+                keep_warm()
             piece = piece_of(s - 1)
             if piece is not None:
                 turn_e(*piece)
@@ -383,13 +395,12 @@ def tile_rbfbias_t_kernel(tc, q, k, v, qs_s, ks_s, alpha, beta, out):
             if piece is not None:
                 second_matmul(*piece)
 
-            g, half = divmod(s + 8, H)
-            if 0 <= g < GROUPS and half < 2:
-                radial(g * H + 2 * half)
+            g = due(s, -8, H, GROUPS)
+            if g is not None:
+                for h in range(H):
+                    radial(g * H + h)
             if 0 <= s + 2 < UNITS:
                 exponent(s + 2)
-            if 0 <= g < GROUPS and half < 2:
-                radial(g * H + 2 * half + 1)
             g = q_due(s - 1)
             if g is not None:
                 copy_q(g)
@@ -412,7 +423,7 @@ def tile_rbfbias_t_kernel(tc, q, k, v, qs_s, ks_s, alpha, beta, out):
             head = k_due(s - 1)
             if head is not None:
                 copy_k(head[0], head[1])
-            g = due(s, 3, H, GROUPS)
+            g = due(s, 4, H, GROUPS)
             if g is not None:
                 reciprocal(g)
             piece = piece_of(s - 3)

@@ -26,6 +26,8 @@ VECTOR_GROUPS = (0,)
 FEATURE_PARTS = (range(0, TILES + 1), range(TILES + 1, SIDES * TILES))
 BANKS = {"scores": 3, "d_sq": 1, "turn": 2, "acc": 2}
 KEEP_WARM = {-12: 2, -11: 1, -10: 1}
+PARAMS = 2
+DERIVED = 4
 POS_PAD = 32
 
 FLOPS = 2 * 2 * B * H * S * S * D
@@ -90,17 +92,21 @@ def tile_rbfbias_t_kernel(tc, q, k, v, qs_s, ks_s, alpha, beta, out):
                 out=pos[:, side, 0 : B * TILES * F].rearrange("p (b x) -> p b x", b=B),
                 in_=source.rearrange("b (p t) f -> p b (t f)", t=TILES),
             )
-        alpha_bf = const.tile([P, H], BF16)
-        nc.scalar.dma_start(out=alpha_bf[:], in_=alpha.rearrange("h o -> (h o)").partition_broadcast(P))
-        beta_bf = const.tile([P, H], BF16)
-        nc.scalar.dma_start(out=beta_bf[:], in_=beta.rearrange("h o -> (h o)").partition_broadcast(P))
+        first_row = const.tile([P, PARAMS, POS_PAD], BF16)
+        for x, source in enumerate((alpha, beta)):
+            nc.scalar.dma_start(out=first_row[0:1, x, 0:H], in_=source.rearrange("h o -> o h"))
+        alpha_row, beta_row = first_row[0:1, 0, 0:H], first_row[0:1, 1, 0:H]
+        row = const.tile([P, DERIVED, H], F32)
+        nc.vector.memset(row[:], 0.0)
+        ones = const.tile([P, P], F32)
+        nc.gpsimd.memset(ones[:], 1.0)
 
         squared = const.tile([P, H], F32)
-        nc.gpsimd.tensor_tensor(out=squared[:], in0=alpha_bf[:], in1=alpha_bf[:], op=ALU.mult)
+        nc.gpsimd.tensor_tensor(out=squared[0:1, :], in0=alpha_row, in1=alpha_row, op=ALU.mult)
         log_squared = const.tile([P, H], F32)
-        nc.scalar.activation(out=log_squared[:], in_=squared[:], func=FUNC.Ln)
+        nc.scalar.activation(out=log_squared[0:1, :], in_=squared[0:1, :], func=FUNC.Ln)
         exp_ready = const.tile([P, H], F32)
-        nc.scalar.activation(out=exp_ready[:], in_=squared[:], func=FUNC.Exp, scale=0.0)
+        nc.scalar.activation(out=exp_ready[0:1, :], in_=squared[0:1, :], func=FUNC.Exp, scale=0.0)
 
         k_raw, q_raw, v_raw, v_grouped = {}, {}, {}, {}
         for s in range(first_step, last_step + 1):
@@ -149,17 +155,18 @@ def tile_rbfbias_t_kernel(tc, q, k, v, qs_s, ks_s, alpha, beta, out):
                     nc.vector.tensor_sub(out=lo, in0=exact, in1=hi)
 
         not_negative = const.tile([P, H], F32)
-        nc.vector.tensor_scalar(out=not_negative[:], in0=alpha_bf[:], scalar1=0.0, scalar2=None, op0=ALU.is_ge)
-        minus_sign = const.tile([P, H], F32)
+        nc.vector.tensor_scalar(out=not_negative[0:1, :], in0=alpha_row, scalar1=0.0, scalar2=None, op0=ALU.is_ge)
         nc.vector.tensor_scalar(
-            out=minus_sign[:], in0=not_negative[:], scalar1=-2.0, scalar2=1.0, op0=ALU.mult, op1=ALU.add
+            out=row[0:1, 0, :], in0=not_negative[0:1, :], scalar1=-2.0, scalar2=1.0, op0=ALU.mult, op1=ALU.add
         )
-        k_scale = const.tile([P, H], F32)
-        nc.vector.tensor_scalar_mul(out=k_scale[:], in0=minus_sign[:], scalar1=-1.0 / math.sqrt(D))
-        log_height = const.tile([P, H], F32)
-        nc.vector.tensor_scalar_mul(out=log_height[:], in0=log_squared[:], scalar1=0.5)
-        two_beta = const.tile([P, H], F32)
-        nc.vector.tensor_scalar_mul(out=two_beta[:], in0=beta_bf[:], scalar1=2.0)
+        nc.vector.tensor_scalar_mul(out=row[0:1, 2, :], in0=beta_row, scalar1=2.0)
+        nc.vector.tensor_scalar_mul(out=row[0:1, 1, :], in0=row[0:1, 0, :], scalar1=-1.0 / math.sqrt(D))
+        nc.vector.tensor_scalar_mul(out=row[0:1, 3, :], in0=log_squared[0:1, :], scalar1=0.5)
+        params = const.tile([P, DERIVED, H], F32)
+        minus_sign = params[:, 0, :]
+        k_scale = params[:, 1, :]
+        two_beta = params[:, 2, :]
+        log_height = params[:, 3, :]
 
         k_ps, k_t, q_ps, q_t, v_codes, v_scales = {}, {}, {}, {}, {}, {}
         d_sq, scores, rbf, minus_z, neg_max, row_sum, inv_sum, e_bf = {}, {}, {}, {}, {}, {}, {}, {}
@@ -178,6 +185,13 @@ def tile_rbfbias_t_kernel(tc, q, k, v, qs_s, ks_s, alpha, beta, out):
                 feat_t[b] = const.tile([P, SIDES * TILES, P], BF16, name="feat_t_%d" % b)
             slots = FEATURE_PARTS[part]
             nc.vector.tensor_copy(out=feat_t[b][:, slots[0] : slots[-1] + 1, :], in_=feat_ps[b, part][:])
+
+        def spread_params():
+            params_ps = psum.tile([P, DERIVED * H], F32, tag="scores", bufs=BANKS["scores"], name="params_ps")
+            nc.tensor.matmul(
+                params_ps[:], lhsT=ones[:], rhs=row[:].rearrange("p x h -> p (x h)"), start=True, stop=True
+            )
+            return params_ps
 
         def turn_k(b, h):
             k_ps[b, h] = psum.tile([P, S], F32, tag="turn", bufs=BANKS["turn"], name="k_ps")
@@ -369,6 +383,8 @@ def tile_rbfbias_t_kernel(tc, q, k, v, qs_s, ks_s, alpha, beta, out):
             piece = piece_of(s - 1)
             if piece is not None:
                 turn_e(*piece)
+            if s == first_step + 1:
+                params_ps = spread_params()
             head = k_due(s)
             if head is not None:
                 turn_k(head[0], head[1])
@@ -420,6 +436,8 @@ def tile_rbfbias_t_kernel(tc, q, k, v, qs_s, ks_s, alpha, beta, out):
                 b = due(s, -11 + 2 * part, UNITS // B, B)
                 if b is not None:
                     copy_features(b, part)
+            if s == first_step + 1:
+                nc.vector.tensor_copy(out=params[:].rearrange("p x h -> p (x h)"), in_=params_ps[:])
             head = k_due(s - 1)
             if head is not None:
                 copy_k(head[0], head[1])

@@ -22,10 +22,12 @@ PAIR = 2
 GROUPS = B * TILES
 UNITS = GROUPS * H
 SIDES = 2
-VECTOR_GROUPS = (0,)
 FEATURE_PARTS = (range(0, TILES + 1), range(TILES + 1, SIDES * TILES))
+K1, Q0, Q1, RAD, DIS, TE = 2, -8, -2, -6, -8, 3
+W1, W2 = 5, 0
+VECTOR_GROUPS = (0, 1)
+FEATURES_DUE = {6: (1, 0), 8: (1, 1)}
 BANKS = {"scores": 3, "d_sq": 1, "turn": 2, "acc": 2}
-KEEP_WARM = {-12: 2, -11: 1, -10: 1}
 PARAMS = 2
 DERIVED = 4
 POS_PAD = 32
@@ -57,34 +59,38 @@ def tile_rbfbias_t_kernel(tc, q, k, v, qs_s, ks_s, alpha, beta, out):
         work = ctx.enter_context(tc.tile_pool(name="work", bufs=2))
         psum = ctx.enter_context(tc.psum_pool(name="psum", bufs=2))
 
-        first_step, last_step = -12, UNITS + 10
+        first_step, last_step = -6, UNITS + 8
 
         def k_due(step):
-            h = due(step, -11, 2, H)
-            if h is not None:
+            if step == first_step:
+                return (0, 0)
+            h = due(step, -5, 1, H)
+            if h is not None and h > 0:
                 return (0, h)
-            h = due(step, -4, H, H)
+            h = due(step, K1, H, H)
             return None if h is None else (1, h)
 
         def q_due(step):
             if step == first_step:
                 return 0
-            g = due(step, -6 - H, H, GROUPS)
-            return None if g is None or g == 0 else g
+            if step == Q1:
+                return 1
+            g = due(step, Q0, H, GROUPS)
+            return None if g is None or g <= 1 else g
 
         def v_due(step):
-            h = due(step, -3, 1, H)
+            h = due(step, -1, 1, H)
             if h is not None:
                 return (0, h)
-            h = due(step, 4, H, H)
+            h = due(step, 6, H, H)
             return None if h is None else (1, h)
 
-        zeros = const.tile([P, S], BF16)
-        nc.gpsimd.memset(zeros[:], 0.0)
-        ident_bf = const.tile([P, P], BF16)
-        make_identity(nc, ident_bf[:])
+        ones = const.tile([P, P], F32)
+        nc.gpsimd.memset(ones[:], 1.0)
         ident_f32 = const.tile([P, P], F32)
         make_identity(nc, ident_f32[:])
+        ident_bf = const.tile([P, P], BF16)
+        make_identity(nc, ident_bf[:])
 
         pos = const.tile([P, SIDES, POS_PAD], BF16)
         for side, (queue, source) in enumerate(((nc.sync, qs_s), (nc.scalar, ks_s))):
@@ -98,28 +104,25 @@ def tile_rbfbias_t_kernel(tc, q, k, v, qs_s, ks_s, alpha, beta, out):
         alpha_row, beta_row = first_row[0:1, 0, 0:H], first_row[0:1, 1, 0:H]
         row = const.tile([P, DERIVED, H], F32)
         nc.vector.memset(row[:], 0.0)
-        ones = const.tile([P, P], F32)
-        nc.gpsimd.memset(ones[:], 1.0)
 
-        squared = const.tile([P, H], F32)
-        nc.gpsimd.tensor_tensor(out=squared[0:1, :], in0=alpha_row, in1=alpha_row, op=ALU.mult)
-        log_squared = const.tile([P, H], F32)
-        nc.scalar.activation(out=log_squared[0:1, :], in_=squared[0:1, :], func=FUNC.Ln)
+        magnitude = const.tile([P, H], F32)
+        nc.scalar.activation(out=magnitude[0:1, :], in_=alpha_row, func=FUNC.Abs)
+        nc.scalar.activation(out=row[0:1, 3, :], in_=magnitude[0:1, :], func=FUNC.Ln, bias=1e-19)
         exp_ready = const.tile([P, H], F32)
-        nc.scalar.activation(out=exp_ready[0:1, :], in_=squared[0:1, :], func=FUNC.Exp, scale=0.0)
+        nc.scalar.activation(out=exp_ready[0:1, :], in_=magnitude[0:1, :], func=FUNC.Exp, scale=0.0)
 
         k_raw, q_raw, v_raw, v_grouped = {}, {}, {}, {}
         for s in range(first_step, last_step + 1):
-            head = k_due(s)
-            if head is not None:
-                k_raw[head] = raw.tile([P, TILES, D], BF16, name="k_raw_%d_%d" % head)
-                nc.sync.dma_start(out=k_raw[head][:], in_=k[head[0], head[1]].rearrange("(p t) d -> p t d", t=TILES))
             g = q_due(s)
             if g is not None:
                 q_raw[g] = raw.tile([P, H, D], BF16, name="q_raw_%d" % g)
                 nc.sync.dma_start(
                     out=q_raw[g][:], in_=q[g // TILES].rearrange("h (p t) d -> t p h d", t=TILES)[g % TILES]
                 )
+            head = k_due(s)
+            if head is not None:
+                k_raw[head] = raw.tile([P, TILES, D], BF16, name="k_raw_%d_%d" % head)
+                nc.sync.dma_start(out=k_raw[head][:], in_=k[head[0], head[1]].rearrange("(p t) d -> p t d", t=TILES))
             head = v_due(s)
             if head is not None:
                 v_raw[head] = raw.tile([P, PACK, D], BF16, name="v_raw_%d_%d" % head)
@@ -161,7 +164,6 @@ def tile_rbfbias_t_kernel(tc, q, k, v, qs_s, ks_s, alpha, beta, out):
         )
         nc.vector.tensor_scalar_mul(out=row[0:1, 2, :], in0=beta_row, scalar1=2.0)
         nc.vector.tensor_scalar_mul(out=row[0:1, 1, :], in0=row[0:1, 0, :], scalar1=-1.0 / math.sqrt(D))
-        nc.vector.tensor_scalar_mul(out=row[0:1, 3, :], in0=log_squared[0:1, :], scalar1=0.5)
         params = const.tile([P, DERIVED, H], F32)
         minus_sign = params[:, 0, :]
         k_scale = params[:, 1, :]
@@ -171,7 +173,7 @@ def tile_rbfbias_t_kernel(tc, q, k, v, qs_s, ks_s, alpha, beta, out):
         k_ps, k_t, q_ps, q_t, v_codes, v_scales = {}, {}, {}, {}, {}, {}
         d_sq, scores, rbf, minus_z, neg_max, row_sum, inv_sum, e_bf = {}, {}, {}, {}, {}, {}, {}, {}
         e_ps, e_grouped, e_codes, e_scales, acc = {}, {}, {}, {}, {}
-        feat_ps, feat_t = {}, {}
+        feat_ps, feat_t, spread_ps = {}, {}, {}
 
         def turn_features(b, part):
             slots = FEATURE_PARTS[part]
@@ -186,12 +188,18 @@ def tile_rbfbias_t_kernel(tc, q, k, v, qs_s, ks_s, alpha, beta, out):
             slots = FEATURE_PARTS[part]
             nc.vector.tensor_copy(out=feat_t[b][:, slots[0] : slots[-1] + 1, :], in_=feat_ps[b, part][:])
 
-        def spread_params():
-            params_ps = psum.tile([P, DERIVED * H], F32, tag="scores", bufs=BANKS["scores"], name="params_ps")
+        def spread(picked):
+            spread_ps[picked.start] = psum.tile([P, picked.stop - picked.start, H], F32, tag="scores", bufs=BANKS["scores"], name="spread_ps")
             nc.tensor.matmul(
-                params_ps[:], lhsT=ones[:], rhs=row[:].rearrange("p x h -> p (x h)"), start=True, stop=True
+                spread_ps[picked.start][:].rearrange("p x h -> p (x h)"),
+                lhsT=ones[:],
+                rhs=row[:, picked, :].rearrange("p x h -> p (x h)"),
+                start=True,
+                stop=True,
             )
-            return params_ps
+
+        def copy_params(picked):
+            nc.vector.tensor_copy(out=params[:, picked, :], in_=spread_ps[picked.start][:])
 
         def turn_k(b, h):
             k_ps[b, h] = psum.tile([P, S], F32, tag="turn", bufs=BANKS["turn"], name="k_ps")
@@ -211,9 +219,9 @@ def tile_rbfbias_t_kernel(tc, q, k, v, qs_s, ks_s, alpha, beta, out):
             for h in range(H):
                 nc.tensor.transpose(q_ps[g][:, h, :], q_raw[g][:, h, :].bitcast(F32), ident_f32[:])
 
-        def copy_q(g):
+        def copy_q(g, copy):
             q_t[g] = work.tile([P, H * P * CHUNKS], BF16, name="q_t", bufs=4)
-            nc.scalar.copy(out=q_t[g][:].bitcast(F32), in_=q_ps[g][:].rearrange("w h i -> w (h i)"))
+            copy(out=q_t[g][:].bitcast(F32), in_=q_ps[g][:].rearrange("w h i -> w (h i)"))
 
         def quantise_v(b, h):
             v_codes[b, h] = operand.tile([P, D], U32, name="v_codes_%d_%d" % (b, h), align_bytes=64)
@@ -225,8 +233,8 @@ def tile_rbfbias_t_kernel(tc, q, k, v, qs_s, ks_s, alpha, beta, out):
             )
 
         def keep_warm():
-            idle = psum.tile([P, S], F32, tag="scores", bufs=BANKS["scores"], name="idle")
-            nc.tensor.matmul(idle[:], lhsT=zeros[:, 0:P], rhs=zeros[:], start=True, stop=True)
+            idle = psum.tile([P, P], F32, tag="scores", bufs=BANKS["scores"], name="idle")
+            nc.tensor.matmul(idle[:], lhsT=ones[:], rhs=ones[:], start=True, stop=True)
 
         def distances(g):
             b, t = divmod(g, TILES)
@@ -377,25 +385,37 @@ def tile_rbfbias_t_kernel(tc, q, k, v, qs_s, ks_s, alpha, beta, out):
                 in_=result[:, 0 : len(heads), :],
             )
 
-        for s in range(first_step, last_step + 1):
-            for extra in range(KEEP_WARM.get(s, 0)):
-                keep_warm()
-            piece = piece_of(s - 1)
+        for i in range(W1):
+            keep_warm()
+        turn_features(0, 0)
+        turn_q(0)
+        spread(slice(0, 4))
+        turn_k(0, 0)
+        copy_features(0, 0)
+        copy_params(slice(0, 4))
+        for i in range(W2):
+            keep_warm()
+        distances(0)
+        turn_features(0, 1)
+        copy_q(0, nc.vector.tensor_copy)
+        copy_k(0, 0)
+        copy_features(0, 1)
+        for h in range(H):
+            radial(h)
+
+        for s in range(first_step + 1, last_step + 1):
+            piece = piece_of(s - TE)
             if piece is not None:
                 turn_e(*piece)
-            if s == first_step + 1:
-                params_ps = spread_params()
             head = k_due(s)
             if head is not None:
                 turn_k(head[0], head[1])
             g = q_due(s)
             if g is not None:
                 turn_q(g)
-            for part in range(2):
-                b = due(s, -12 + 2 * part, UNITS // B, B)
-                if b is not None:
-                    turn_features(b, part)
-            u = s + 6
+            if s in FEATURES_DUE:
+                turn_features(*FEATURES_DUE[s])
+            u = s + 4
             if 0 <= u < UNITS:
                 scores[u] = psum.tile([P, S], F32, tag="scores", bufs=BANKS["scores"], name="scores")
                 if u % 2 == 0:
@@ -404,50 +424,46 @@ def tile_rbfbias_t_kernel(tc, q, k, v, qs_s, ks_s, alpha, beta, out):
                 else:
                     first_matmul(u)
                     add_bias(u)
-            g = due(s, -10, H, GROUPS)
-            if g is not None:
+            g = due(s, DIS, H, GROUPS)
+            if g is not None and g > 0:
                 distances(g)
-            piece = piece_of(s - 5)
+            piece = piece_of(s - TE - 4)
             if piece is not None:
                 second_matmul(*piece)
 
-            g = due(s, -8, H, GROUPS)
-            if g is not None:
+            g = due(s, RAD, H, GROUPS)
+            if g is not None and g > 0:
                 for h in range(H):
                     radial(g * H + h)
-            if 0 <= s + 2 < UNITS:
-                exponent(s + 2)
+            if 0 <= s < UNITS:
+                exponent(s)
             g = q_due(s - 1)
-            if g is not None:
-                copy_q(g)
-            piece = piece_of(s - 2)
+            if g is not None and g > 0:
+                copy_q(g, nc.scalar.copy)
+            piece = piece_of(s - TE - 1)
             if piece is not None and piece[0] == GROUPS - 1:
                 copy_e(*piece, nc.scalar.copy)
-            piece = piece_of(s - 6)
+            piece = piece_of(s - TE - 5)
             if piece is not None and H - 1 not in piece[1]:
                 normalise(*piece)
 
-            piece = piece_of(s - 2)
+            piece = piece_of(s - TE - 1)
             if piece is not None and piece[0] < GROUPS - 1:
                 copy_e(*piece, nc.vector.tensor_copy)
-            if 0 <= s + 4 < UNITS:
-                logits(s + 4)
-            for part in range(2):
-                b = due(s, -11 + 2 * part, UNITS // B, B)
-                if b is not None:
-                    copy_features(b, part)
-            if s == first_step + 1:
-                nc.vector.tensor_copy(out=params[:].rearrange("p x h -> p (x h)"), in_=params_ps[:])
-            head = k_due(s - 1)
-            if head is not None:
+            if 0 <= s + 2 < UNITS:
+                logits(s + 2)
+            if s - 1 in FEATURES_DUE:
+                copy_features(*FEATURES_DUE[s - 1])
+            head = k_due(s)
+            if head is not None and head != (0, 0):
                 copy_k(head[0], head[1])
-            g = due(s, 4, H, GROUPS)
+            g = due(s, 6, H, GROUPS)
             if g is not None:
                 reciprocal(g)
-            piece = piece_of(s - 3)
+            piece = piece_of(s - TE - 2)
             if piece is not None:
                 quantise_e(*piece)
-            piece = piece_of(s - 6)
+            piece = piece_of(s - TE - 5)
             if piece is not None and H - 1 in piece[1]:
                 normalise(*piece)
             head = v_due(s - 7)

@@ -23,9 +23,29 @@ GROUPS = B * TILES
 UNITS = GROUPS * H
 SIDES = 2
 FEATURE_PARTS = (range(0, TILES + 1), range(TILES + 1, SIDES * TILES))
-K1, Q0, Q1, RAD, DIS, TE = 2, -8, -2, -6, -8, 3
-W1, W2 = 5, 0
-VECTOR_GROUPS = (0, 1)
+K1, Q0, Q1, RAD, DIS, TE = 2, -8, -3, -5, -6, 3
+W1, W2 = 0, 0
+KB0, FIRST = -6, -6
+CQ, CK, AD, QV = 0, 0, 1, 4
+
+CL, NL = 1, (0, 2, 3)
+MX, CE, QU, NO, EXTRA, VO, RE, SC, SN = 7, 4, 5, 8, 0, 0, 5, 0, 1
+
+def q_on_vector(g):
+    return g < QV
+
+
+def copied_by_scalar(g, heads):
+    return g == GROUPS - 1 and CL or g < SC and 0 in heads
+
+
+def normalised_by_scalar(g, heads):
+    return H - 1 not in heads if g < GROUPS - 1 else heads[0] in NL
+
+
+LEAD, LL, BIAS_FIRST, EXPFIRST = 4, 2, 0, 0
+DIS1, RAD1 = {-3: 1}, {-3: 1}
+VECTOR_GROUPS = (0,)
 FEATURES_DUE = {6: (1, 0), 8: (1, 1)}
 BANKS = {"scores": 3, "d_sq": 1, "turn": 2, "acc": 2}
 PARAMS = 2
@@ -40,13 +60,16 @@ def due(step, first, every, count):
     return n if rest == 0 and 0 <= n < count else None
 
 
-def piece_of(step):
-    if not 0 <= step < UNITS:
-        return None
-    g, h = divmod(step, H)
-    if step >= UNITS - PAIR:
-        return g, range(h, h + 1)
-    return (g, range(h - 1, h + 1)) if h % PAIR == 1 else None
+def pieces_due(step, lag):
+    found = []
+    for g in range(GROUPS):
+        cuts = (2, 1, 1) if g == GROUPS - 1 else (2, 2)
+        h = 0
+        for n in cuts:
+            if g * H + h + n - 1 + lag + (0 if g == GROUPS - 1 else EXTRA) == step:
+                found.append((g, range(h, h + n)))
+            h += n
+    return found
 
 
 def tile_rbfbias_t_kernel(tc, q, k, v, qs_s, ks_s, alpha, beta, out):
@@ -59,12 +82,12 @@ def tile_rbfbias_t_kernel(tc, q, k, v, qs_s, ks_s, alpha, beta, out):
         work = ctx.enter_context(tc.tile_pool(name="work", bufs=2))
         psum = ctx.enter_context(tc.psum_pool(name="psum", bufs=2))
 
-        first_step, last_step = -6, UNITS + 8
+        first_step, last_step = FIRST, UNITS + 18
 
         def k_due(step):
             if step == first_step:
                 return (0, 0)
-            h = due(step, -5, 1, H)
+            h = due(step, KB0, 1, H)
             if h is not None and h > 0:
                 return (0, h)
             h = due(step, K1, H, H)
@@ -106,10 +129,6 @@ def tile_rbfbias_t_kernel(tc, q, k, v, qs_s, ks_s, alpha, beta, out):
         nc.vector.memset(row[:], 0.0)
 
         magnitude = const.tile([P, H], F32)
-        nc.scalar.activation(out=magnitude[0:1, :], in_=alpha_row, func=FUNC.Abs)
-        nc.scalar.activation(out=row[0:1, 3, :], in_=magnitude[0:1, :], func=FUNC.Ln, bias=1e-19)
-        exp_ready = const.tile([P, H], F32)
-        nc.scalar.activation(out=exp_ready[0:1, :], in_=magnitude[0:1, :], func=FUNC.Exp, scale=0.0)
 
         k_raw, q_raw, v_raw, v_grouped = {}, {}, {}, {}
         for s in range(first_step, last_step + 1):
@@ -147,18 +166,21 @@ def tile_rbfbias_t_kernel(tc, q, k, v, qs_s, ks_s, alpha, beta, out):
         half_square = const.tile([P, SIDES, B * TILES * F], F32)
         nc.vector.scalar_tensor_tensor(out=half_square[:], in0=x, scalar=-0.5, in1=x, op0=ALU.mult, op1=ALU.mult)
         nc.vector.tensor_copy(out=feat[:, :, :, 0:F], in_=x.rearrange("p s (x f) -> p s x f", f=F))
-        for part in range(2):
-            for side in range(SIDES):
-                exact = half_square[:, side, :].rearrange("p (x f) -> p x f", f=F)
-                hi = feat[:, side, :, square_at[side] : square_at[side] + F]
-                if part == 0:
-                    nc.vector.tensor_copy(out=hi, in_=exact)
-                else:
-                    lo = feat[:, side, :, square_at[side] + F : square_at[side] + 2 * F]
-                    nc.vector.tensor_sub(out=lo, in0=exact, in1=hi)
-
+        nc.vector.scalar_tensor_tensor(
+            out=magnitude[0:1, :], in0=alpha_row, scalar=-1.0, in1=alpha_row, op0=ALU.mult, op1=ALU.max
+        )
+        nc.scalar.activation(out=row[0:1, 3, :], in_=magnitude[0:1, :], func=FUNC.Ln, bias=1e-19)
+        exp_ready = const.tile([P, H], F32)
+        nc.scalar.activation(out=exp_ready[0:1, :], in_=magnitude[0:1, :], func=FUNC.Exp, scale=0.0)
+        exact = [half_square[:, side, :].rearrange("p (x f) -> p x f", f=F) for side in range(SIDES)]
+        hi = [feat[:, side, :, square_at[side] : square_at[side] + F] for side in range(SIDES)]
+        lo = [feat[:, side, :, square_at[side] + F : square_at[side] + 2 * F] for side in range(SIDES)]
+        for side in range(SIDES):
+            nc.vector.tensor_copy(out=hi[side], in_=exact[side])
         not_negative = const.tile([P, H], F32)
         nc.vector.tensor_scalar(out=not_negative[0:1, :], in0=alpha_row, scalar1=0.0, scalar2=None, op0=ALU.is_ge)
+        for side in range(SIDES):
+            nc.vector.tensor_sub(out=lo[side], in0=exact[side], in1=hi[side])
         nc.vector.tensor_scalar(
             out=row[0:1, 0, :], in0=not_negative[0:1, :], scalar1=-2.0, scalar2=1.0, op0=ALU.mult, op1=ALU.add
         )
@@ -173,7 +195,7 @@ def tile_rbfbias_t_kernel(tc, q, k, v, qs_s, ks_s, alpha, beta, out):
         k_ps, k_t, q_ps, q_t, v_codes, v_scales = {}, {}, {}, {}, {}, {}
         d_sq, scores, rbf, minus_z, neg_max, row_sum, inv_sum, e_bf = {}, {}, {}, {}, {}, {}, {}, {}
         e_ps, e_grouped, e_codes, e_scales, acc = {}, {}, {}, {}, {}
-        feat_ps, feat_t, spread_ps = {}, {}, {}
+        feat_ps, feat_t, spread_ps, total = {}, {}, {}, {}
 
         def turn_features(b, part):
             slots = FEATURE_PARTS[part]
@@ -267,8 +289,8 @@ def tile_rbfbias_t_kernel(tc, q, k, v, qs_s, ks_s, alpha, beta, out):
                     scores[u][:],
                     lhsT=q_heads[:, h, :, c],
                     rhs=k_t[g // TILES, h][:, :, c],
-                    start=(c == 0 and (u % 2 == 1 or g in VECTOR_GROUPS)),
-                    stop=(c == CHUNKS - 1 and (u % 2 == 0 or g in VECTOR_GROUPS)),
+                    start=(c == 0 and (u % 2 != BIAS_FIRST or g in VECTOR_GROUPS)),
+                    stop=(c == CHUNKS - 1 and (u % 2 == BIAS_FIRST or g in VECTOR_GROUPS)),
                 )
 
         def add_bias(u):
@@ -280,22 +302,23 @@ def tile_rbfbias_t_kernel(tc, q, k, v, qs_s, ks_s, alpha, beta, out):
                     lhsT=rbf[u][:, c * P : (c + 1) * P],
                     rhs=ident_f32[:],
                     is_transpose=True,
-                    start=(u % 2 == 0 and c == 0),
-                    stop=(u % 2 == 1 and c == TILES - 1),
+                    start=(u % 2 == BIAS_FIRST and c == 0),
+                    stop=(u % 2 != BIAS_FIRST and c == TILES - 1),
                 )
+
+        def add_on_vector(u):
+            if u // H in VECTOR_GROUPS:
+                total[u] = work.tile([P, S], F32, name="total", bufs=3)
+                nc.vector.tensor_add(out=total[u][:], in0=rbf[u][:], in1=scores[u][:])
 
         def logits(u):
             g, h = divmod(u, H)
             if h == 0:
                 neg_max[g] = work.tile([P, H], F32, name="neg_max", bufs=3)
             minus_z[u] = work.tile([P, S], F32, name="minus_z", bufs=8)
-            total = scores[u]
-            if g in VECTOR_GROUPS:
-                total = work.tile([P, S], F32, name="total", bufs=3)
-                nc.vector.tensor_add(out=total[:], in0=rbf[u][:], in1=scores[u][:])
             nc.vector.tensor_scalar(
                 out=minus_z[u][:],
-                in0=total[:],
+                in0=(total[u] if g in VECTOR_GROUPS else scores[u])[:],
                 scalar1=minus_sign[:, h : h + 1],
                 scalar2=None,
                 op0=ALU.mult,
@@ -369,7 +392,7 @@ def tile_rbfbias_t_kernel(tc, q, k, v, qs_s, ks_s, alpha, beta, out):
             b, t = divmod(g, TILES)
             result = work.tile([P, PAIR, D], F32, bufs=6)
             inv = inv_sum[g][:, heads[0] : heads[0] + len(heads)]
-            if H - 1 in heads:
+            if not normalised_by_scalar(g, heads):
                 nc.vector.tensor_mul(
                     out=result[:, 0 : len(heads), :],
                     in0=acc[g, heads][:, 0 : len(heads), :],
@@ -385,10 +408,18 @@ def tile_rbfbias_t_kernel(tc, q, k, v, qs_s, ks_s, alpha, beta, out):
                 in_=result[:, 0 : len(heads), :],
             )
 
+        def logits_step(s):
+            if AD and 0 <= s + LL + AD < UNITS:
+                add_on_vector(s + LL + AD)
+            if 0 <= s + LL < UNITS:
+                if not AD:
+                    add_on_vector(s + LL)
+                logits(s + LL)
+
         for i in range(W1):
             keep_warm()
-        turn_features(0, 0)
         turn_q(0)
+        turn_features(0, 0)
         spread(slice(0, 4))
         turn_k(0, 0)
         copy_features(0, 0)
@@ -404,8 +435,7 @@ def tile_rbfbias_t_kernel(tc, q, k, v, qs_s, ks_s, alpha, beta, out):
             radial(h)
 
         for s in range(first_step + 1, last_step + 1):
-            piece = piece_of(s - TE)
-            if piece is not None:
+            for piece in pieces_due(s, TE):
                 turn_e(*piece)
             head = k_due(s)
             if head is not None:
@@ -415,57 +445,62 @@ def tile_rbfbias_t_kernel(tc, q, k, v, qs_s, ks_s, alpha, beta, out):
                 turn_q(g)
             if s in FEATURES_DUE:
                 turn_features(*FEATURES_DUE[s])
-            u = s + 4
+            u = s + LEAD
             if 0 <= u < UNITS:
                 scores[u] = psum.tile([P, S], F32, tag="scores", bufs=BANKS["scores"], name="scores")
-                if u % 2 == 0:
+                if u % 2 == BIAS_FIRST:
                     add_bias(u)
                     first_matmul(u)
                 else:
                     first_matmul(u)
                     add_bias(u)
-            g = due(s, DIS, H, GROUPS)
-            if g is not None and g > 0:
+            g = DIS1.get(s, due(s, DIS, H, GROUPS))
+            if g is not None and (g > 1 or s in DIS1):
                 distances(g)
-            piece = piece_of(s - TE - 4)
-            if piece is not None:
+            for piece in pieces_due(s, MX):
                 second_matmul(*piece)
 
-            g = due(s, RAD, H, GROUPS)
-            if g is not None and g > 0:
+            if EXPFIRST and 0 <= s < UNITS:
+                exponent(s)
+            g = RAD1.get(s, due(s, RAD, H, GROUPS))
+            if g is not None and (g > 1 or s in RAD1):
                 for h in range(H):
                     radial(g * H + h)
-            if 0 <= s < UNITS:
+            if not EXPFIRST and 0 <= s < UNITS:
                 exponent(s)
-            g = q_due(s - 1)
-            if g is not None and g > 0:
+            g = q_due(s - CQ)
+            if g is not None and g > 0 and not q_on_vector(g):
                 copy_q(g, nc.scalar.copy)
-            piece = piece_of(s - TE - 1)
-            if piece is not None and piece[0] == GROUPS - 1:
-                copy_e(*piece, nc.scalar.copy)
-            piece = piece_of(s - TE - 5)
-            if piece is not None and H - 1 not in piece[1]:
-                normalise(*piece)
+            for piece in pieces_due(s, CE):
+                if copied_by_scalar(*piece):
+                    copy_e(*piece, nc.scalar.copy)
+            for piece in pieces_due(s, NO):
+                if normalised_by_scalar(*piece):
+                    normalise(*piece)
 
-            piece = piece_of(s - TE - 1)
-            if piece is not None and piece[0] < GROUPS - 1:
-                copy_e(*piece, nc.vector.tensor_copy)
-            if 0 <= s + 2 < UNITS:
-                logits(s + 2)
+            if VO:
+                logits_step(s)
+            for piece in pieces_due(s, CE):
+                if not copied_by_scalar(*piece):
+                    copy_e(*piece, nc.vector.tensor_copy)
+            if not VO:
+                logits_step(s)
             if s - 1 in FEATURES_DUE:
                 copy_features(*FEATURES_DUE[s - 1])
-            head = k_due(s)
+            head = k_due(s - CK)
             if head is not None and head != (0, 0):
                 copy_k(head[0], head[1])
-            g = due(s, 6, H, GROUPS)
+            g = q_due(s)
+            if g is not None and g > 0 and q_on_vector(g):
+                copy_q(g, nc.vector.tensor_copy)
+            g = due(s, RE, H, GROUPS)
             if g is not None:
                 reciprocal(g)
-            piece = piece_of(s - TE - 2)
-            if piece is not None:
+            for piece in pieces_due(s, QU):
                 quantise_e(*piece)
-            piece = piece_of(s - TE - 5)
-            if piece is not None and H - 1 in piece[1]:
-                normalise(*piece)
+            for piece in pieces_due(s, NO):
+                if not normalised_by_scalar(*piece):
+                    normalise(*piece)
             head = v_due(s - 7)
             if head is not None:
                 quantise_v(head[0], head[1])

@@ -23,30 +23,31 @@ GROUPS = B * TILES
 UNITS = GROUPS * H
 SIDES = 2
 FEATURE_PARTS = (range(0, TILES + 1), range(TILES + 1, SIDES * TILES))
-K1, Q0, Q1, RAD, DIS, TE = 2, -8, -3, -5, -6, 3
-W1, W2 = 0, 0
+K1, Q0, Q1, RAD, DIS, TE = -2, -8, -3, -6, -8, 3
+W1, W2 = 5, 0
 KB0, FIRST = -6, -6
-CQ, CK, AD, QV = 0, 0, 1, 4
+CQ, CK, AD, QV = 0, 0, 1, 1
 
-CL, NL = 1, (0, 2, 3)
-MX, CE, QU, NO, EXTRA, VO, RE, SC, SN = 7, 4, 5, 8, 0, 0, 5, 0, 1
+CL, NL = (0, 2, 3), (0, 2)
+FS, KF, QF, MXE, TL, SC0, NS0, NS = 0, 0, 1, 0, 1, 1, 2, 5
+MX, CE, QU, NO, EXTRA, VO, RE, SC, SN = 7, 4, 6, 9, 0, 0, 7, 0, 1
 
 def q_on_vector(g):
     return g < QV
 
 
 def copied_by_scalar(g, heads):
-    return g == GROUPS - 1 and CL or g < SC and 0 in heads
+    return g == GROUPS - 1 and heads[0] in CL or SC0 <= g < SC and 0 in heads
 
 
 def normalised_by_scalar(g, heads):
-    return H - 1 not in heads if g < GROUPS - 1 else heads[0] in NL
+    return (H - 1 not in heads or NS0 <= g < NS) if g < GROUPS - 1 else heads[0] in NL
 
 
-LEAD, LL, BIAS_FIRST, EXPFIRST = 4, 2, 0, 0
-DIS1, RAD1 = {-3: 1}, {-3: 1}
-VECTOR_GROUPS = (0,)
-FEATURES_DUE = {6: (1, 0), 8: (1, 1)}
+LEAD, LL, BIAS_FIRST, EXPFIRST = 4, 2, 0, 1
+DIS1, RAD1 = {-3: 1}, {-1: 1}
+VECTOR_GROUPS = (0,1,5)
+FEATURES_DUE = {2: (1, 0), 4: (1, 1)}
 BANKS = {"scores": 3, "d_sq": 1, "turn": 2, "acc": 2}
 PARAMS = 2
 DERIVED = 4
@@ -435,8 +436,9 @@ def tile_rbfbias_t_kernel(tc, q, k, v, qs_s, ks_s, alpha, beta, out):
             radial(h)
 
         for s in range(first_step + 1, last_step + 1):
-            for piece in pieces_due(s, TE):
-                turn_e(*piece)
+            if not TL:
+                for piece in pieces_due(s, TE):
+                    turn_e(*piece)
             head = k_due(s)
             if head is not None:
                 turn_k(head[0], head[1])
@@ -445,11 +447,17 @@ def tile_rbfbias_t_kernel(tc, q, k, v, qs_s, ks_s, alpha, beta, out):
                 turn_q(g)
             if s in FEATURES_DUE:
                 turn_features(*FEATURES_DUE[s])
+            if TL:
+                for piece in pieces_due(s, TE):
+                    turn_e(*piece)
             u = s + LEAD
             if 0 <= u < UNITS:
                 scores[u] = psum.tile([P, S], F32, tag="scores", bufs=BANKS["scores"], name="scores")
                 if u % 2 == BIAS_FIRST:
                     add_bias(u)
+                    if MXE:
+                        for piece in pieces_due(s, MX):
+                            second_matmul(*piece)
                     first_matmul(u)
                 else:
                     first_matmul(u)
@@ -457,8 +465,9 @@ def tile_rbfbias_t_kernel(tc, q, k, v, qs_s, ks_s, alpha, beta, out):
             g = DIS1.get(s, due(s, DIS, H, GROUPS))
             if g is not None and (g > 1 or s in DIS1):
                 distances(g)
-            for piece in pieces_due(s, MX):
-                second_matmul(*piece)
+            if not (MXE and 0 <= u < UNITS and u % 2 == BIAS_FIRST):
+                for piece in pieces_due(s, MX):
+                    second_matmul(*piece)
 
             if EXPFIRST and 0 <= s < UNITS:
                 exponent(s)
@@ -478,6 +487,12 @@ def tile_rbfbias_t_kernel(tc, q, k, v, qs_s, ks_s, alpha, beta, out):
                 if normalised_by_scalar(*piece):
                     normalise(*piece)
 
+            head = k_due(s - CK)
+            if head is not None and head != (0, 0) and KF:
+                copy_k(head[0], head[1])
+            if QF:
+                for piece in pieces_due(s, QU):
+                    quantise_e(*piece)
             if VO:
                 logits_step(s)
             for piece in pieces_due(s, CE):
@@ -485,10 +500,10 @@ def tile_rbfbias_t_kernel(tc, q, k, v, qs_s, ks_s, alpha, beta, out):
                     copy_e(*piece, nc.vector.tensor_copy)
             if not VO:
                 logits_step(s)
-            if s - 1 in FEATURES_DUE:
-                copy_features(*FEATURES_DUE[s - 1])
+            if s - FS in FEATURES_DUE:
+                copy_features(*FEATURES_DUE[s - FS])
             head = k_due(s - CK)
-            if head is not None and head != (0, 0):
+            if head is not None and head != (0, 0) and not KF:
                 copy_k(head[0], head[1])
             g = q_due(s)
             if g is not None and g > 0 and q_on_vector(g):
@@ -496,8 +511,9 @@ def tile_rbfbias_t_kernel(tc, q, k, v, qs_s, ks_s, alpha, beta, out):
             g = due(s, RE, H, GROUPS)
             if g is not None:
                 reciprocal(g)
-            for piece in pieces_due(s, QU):
-                quantise_e(*piece)
+            if not QF:
+                for piece in pieces_due(s, QU):
+                    quantise_e(*piece)
             for piece in pieces_due(s, NO):
                 if not normalised_by_scalar(*piece):
                     normalise(*piece)

import math
from contextlib import ExitStack

import concourse.mybir as mybir
from concourse.masks import make_identity

F32 = mybir.dt.float32
BF16 = mybir.dt.bfloat16
U32 = mybir.dt.uint32
U8 = mybir.dt.uint8
FP8X4 = mybir.dt.float8_e4m3fn_x4
ALU = mybir.AluOpType
FUNC = mybir.ActivationFunctionType

B, H, S, D, F = 2, 4, 512, 256, 3
P = 128
TILES = S // P
CHUNKS = D // P
PACK = 4
HALVES = 2
PAIR = 2
GROUPS = B * TILES
UNITS = GROUPS * H
SIDES = 2
FEATURE_PARTS = (range(0, TILES + 1), range(TILES + 1, SIDES * TILES))
K1, Q0, Q1, RAD, DIS, TE = -2, -8, -3, -6, -8, 3
W1, W2 = 5, 0
KB0, FIRST = -6, -6
CQ, CK, AD, QV = 0, 0, 1, 1

CL, NL = (0, 2, 3), (0, 2)
FS, KF, QF, MXE, TL, SC0, NS0, NS = 0, 0, 1, 0, 1, 1, 2, 5
MX, CE, QU, NO, EXTRA, VO, RE, SC, SN = 7, 4, 6, 9, 0, 0, 7, 0, 1

def q_on_vector(g):
    return g < QV


def copied_by_scalar(g, heads):
    return g == GROUPS - 1 and heads[0] in CL or SC0 <= g < SC and 0 in heads


def normalised_by_scalar(g, heads):
    return (H - 1 not in heads or NS0 <= g < NS) if g < GROUPS - 1 else heads[0] in NL


LEAD, LL, BIAS_FIRST, EXPFIRST = 4, 2, 0, 1
DIS1, RAD1 = {-3: 1}, {-1: 1}
VECTOR_GROUPS = (0,1,5)
FEATURES_DUE = {2: (1, 0), 4: (1, 1)}
BANKS = {"scores": 3, "d_sq": 1, "turn": 2, "acc": 2}
PARAMS = 2
DERIVED = 4
POS_PAD = 32

FLOPS = 2 * 2 * B * H * S * S * D


def due(step, first, every, count):
    n, rest = divmod(step - first, every)
    return n if rest == 0 and 0 <= n < count else None


def pieces_due(step, lag):
    found = []
    for g in range(GROUPS):
        cuts = (2, 1, 1) if g == GROUPS - 1 else (2, 2)
        h = 0
        for n in cuts:
            if g * H + h + n - 1 + lag + (0 if g == GROUPS - 1 else EXTRA) == step:
                found.append((g, range(h, h + n)))
            h += n
    return found


def tile_rbfbias_t_kernel(tc, q, k, v, qs_s, ks_s, alpha, beta, out):
    nc = tc.nc
    with ExitStack() as ctx:
        ctx.enter_context(tc.manual_schedule())
        const = ctx.enter_context(tc.tile_pool(name="const", bufs=1))
        raw = ctx.enter_context(tc.tile_pool(name="raw", bufs=1))
        operand = ctx.enter_context(tc.tile_pool(name="operand", bufs=1))
        work = ctx.enter_context(tc.tile_pool(name="work", bufs=2))
        psum = ctx.enter_context(tc.psum_pool(name="psum", bufs=2))

        first_step, last_step = FIRST, UNITS + 18

        def k_due(step):
            if step == first_step:
                return (0, 0)
            h = due(step, KB0, 1, H)
            if h is not None and h > 0:
                return (0, h)
            h = due(step, K1, H, H)
            return None if h is None else (1, h)

        def q_due(step):
            if step == first_step:
                return 0
            if step == Q1:
                return 1
            g = due(step, Q0, H, GROUPS)
            return None if g is None or g <= 1 else g

        def v_due(step):
            h = due(step, -1, 1, H)
            if h is not None:
                return (0, h)
            h = due(step, 6, H, H)
            return None if h is None else (1, h)

        ones = const.tile([P, P], F32)
        nc.gpsimd.memset(ones[:], 1.0)
        ident_f32 = const.tile([P, P], F32)
        make_identity(nc, ident_f32[:])
        ident_bf = const.tile([P, P], BF16)
        make_identity(nc, ident_bf[:])

        pos = const.tile([P, SIDES, POS_PAD], BF16)
        for side, (queue, source) in enumerate(((nc.sync, qs_s), (nc.scalar, ks_s))):
            queue.dma_start(
                out=pos[:, side, 0 : B * TILES * F].rearrange("p (b x) -> p b x", b=B),
                in_=source.rearrange("b (p t) f -> p b (t f)", t=TILES),
            )
        first_row = const.tile([P, PARAMS, POS_PAD], BF16)
        for x, source in enumerate((alpha, beta)):
            nc.scalar.dma_start(out=first_row[0:1, x, 0:H], in_=source.rearrange("h o -> o h"))
        alpha_row, beta_row = first_row[0:1, 0, 0:H], first_row[0:1, 1, 0:H]
        row = const.tile([P, DERIVED, H], F32)
        nc.vector.memset(row[:], 0.0)

        magnitude = const.tile([P, H], F32)

        k_raw, q_raw, v_raw, v_grouped = {}, {}, {}, {}
        for s in range(first_step, last_step + 1):
            g = q_due(s)
            if g is not None:
                q_raw[g] = raw.tile([P, H, D], BF16, name="q_raw_%d" % g)
                nc.sync.dma_start(
                    out=q_raw[g][:], in_=q[g // TILES].rearrange("h (p t) d -> t p h d", t=TILES)[g % TILES]
                )
            head = k_due(s)
            if head is not None:
                k_raw[head] = raw.tile([P, TILES, D], BF16, name="k_raw_%d_%d" % head)
                nc.sync.dma_start(out=k_raw[head][:], in_=k[head[0], head[1]].rearrange("(p t) d -> p t d", t=TILES))
            head = v_due(s)
            if head is not None:
                v_raw[head] = raw.tile([P, PACK, D], BF16, name="v_raw_%d_%d" % head)
                nc.sync.dma_start(out=v_raw[head][:], in_=v[head[0], head[1]].rearrange("(p r) d -> p r d", r=PACK))
                v_grouped[head] = operand.tile([P, D, PACK], BF16, name="v_grouped_%d_%d" % head, align_bytes=64)
                nc.gpsimd.tensor_scalar(
                    out=v_grouped[head][:],
                    in0=v_raw[head][:].rearrange("p r d -> p d r"),
                    scalar1=1.0,
                    scalar2=0.0,
                    op0=ALU.mult,
                    op1=ALU.add,
                )

        square_at = (F, 3 * F)
        ones_at = (3 * F, F)
        feat = const.tile([P, SIDES, B * TILES, P], BF16)
        nc.vector.memset(feat[:], 0.0)
        for side in range(SIDES):
            nc.vector.memset(feat[:, side, :, ones_at[side] : ones_at[side] + 2 * F], 1.0)
        x = pos[:, :, 0 : B * TILES * F]
        half_square = const.tile([P, SIDES, B * TILES * F], F32)
        nc.vector.scalar_tensor_tensor(out=half_square[:], in0=x, scalar=-0.5, in1=x, op0=ALU.mult, op1=ALU.mult)
        nc.vector.tensor_copy(out=feat[:, :, :, 0:F], in_=x.rearrange("p s (x f) -> p s x f", f=F))
        nc.vector.scalar_tensor_tensor(
            out=magnitude[0:1, :], in0=alpha_row, scalar=-1.0, in1=alpha_row, op0=ALU.mult, op1=ALU.max
        )
        nc.scalar.activation(out=row[0:1, 3, :], in_=magnitude[0:1, :], func=FUNC.Ln, bias=1e-19)
        exp_ready = const.tile([P, H], F32)
        nc.scalar.activation(out=exp_ready[0:1, :], in_=magnitude[0:1, :], func=FUNC.Exp, scale=0.0)
        exact = [half_square[:, side, :].rearrange("p (x f) -> p x f", f=F) for side in range(SIDES)]
        hi = [feat[:, side, :, square_at[side] : square_at[side] + F] for side in range(SIDES)]
        lo = [feat[:, side, :, square_at[side] + F : square_at[side] + 2 * F] for side in range(SIDES)]
        for side in range(SIDES):
            nc.vector.tensor_copy(out=hi[side], in_=exact[side])
        not_negative = const.tile([P, H], F32)
        nc.vector.tensor_scalar(out=not_negative[0:1, :], in0=alpha_row, scalar1=0.0, scalar2=None, op0=ALU.is_ge)
        for side in range(SIDES):
            nc.vector.tensor_sub(out=lo[side], in0=exact[side], in1=hi[side])
        nc.vector.tensor_scalar(
            out=row[0:1, 0, :], in0=not_negative[0:1, :], scalar1=-2.0, scalar2=1.0, op0=ALU.mult, op1=ALU.add
        )
        nc.vector.tensor_scalar_mul(out=row[0:1, 2, :], in0=beta_row, scalar1=2.0)
        nc.vector.tensor_scalar_mul(out=row[0:1, 1, :], in0=row[0:1, 0, :], scalar1=-1.0 / math.sqrt(D))
        params = const.tile([P, DERIVED, H], F32)
        minus_sign = params[:, 0, :]
        k_scale = params[:, 1, :]
        two_beta = params[:, 2, :]
        log_height = params[:, 3, :]

        k_ps, k_t, q_ps, q_t, v_codes, v_scales = {}, {}, {}, {}, {}, {}
        d_sq, scores, rbf, minus_z, neg_max, row_sum, inv_sum, e_bf = {}, {}, {}, {}, {}, {}, {}, {}
        e_ps, e_grouped, e_codes, e_scales, acc = {}, {}, {}, {}, {}
        feat_ps, feat_t, spread_ps, total = {}, {}, {}, {}

        def turn_features(b, part):
            slots = FEATURE_PARTS[part]
            feat_ps[b, part] = psum.tile([P, len(slots), P], BF16, tag="acc", bufs=BANKS["acc"], name="feat_ps")
            for x, slot in enumerate(slots):
                side, t = 1 - slot // TILES, slot % TILES
                nc.tensor.transpose(feat_ps[b, part][:, x, :], feat[:, side, b * TILES + t, :], ident_bf[:])

        def copy_features(b, part):
            if part == 0:
                feat_t[b] = const.tile([P, SIDES * TILES, P], BF16, name="feat_t_%d" % b)
            slots = FEATURE_PARTS[part]
            nc.vector.tensor_copy(out=feat_t[b][:, slots[0] : slots[-1] + 1, :], in_=feat_ps[b, part][:])

        def spread(picked):
            spread_ps[picked.start] = psum.tile([P, picked.stop - picked.start, H], F32, tag="scores", bufs=BANKS["scores"], name="spread_ps")
            nc.tensor.matmul(
                spread_ps[picked.start][:].rearrange("p x h -> p (x h)"),
                lhsT=ones[:],
                rhs=row[:, picked, :].rearrange("p x h -> p (x h)"),
                start=True,
                stop=True,
            )

        def copy_params(picked):
            nc.vector.tensor_copy(out=params[:, picked, :], in_=spread_ps[picked.start][:])

        def turn_k(b, h):
            k_ps[b, h] = psum.tile([P, S], F32, tag="turn", bufs=BANKS["turn"], name="k_ps")
            for t in range(TILES):
                nc.tensor.transpose(k_ps[b, h][:, t * P : (t + 1) * P], k_raw[b, h][:, t, :].bitcast(F32), ident_f32[:])

        def copy_k(b, h):
            k_t[b, h] = operand.tile([P, S, CHUNKS], BF16, name="k_t_%d_%d" % (b, h))
            nc.vector.tensor_scalar_mul(
                out=k_t[b, h][:].rearrange("w j c -> w (j c)"),
                in0=k_ps[b, h][:].bitcast(BF16),
                scalar1=k_scale[:, h : h + 1],
            )

        def turn_q(g):
            q_ps[g] = psum.tile([P, H, P], F32, tag="turn", bufs=BANKS["turn"], name="q_ps")
            for h in range(H):
                nc.tensor.transpose(q_ps[g][:, h, :], q_raw[g][:, h, :].bitcast(F32), ident_f32[:])

        def copy_q(g, copy):
            q_t[g] = work.tile([P, H * P * CHUNKS], BF16, name="q_t", bufs=4)
            copy(out=q_t[g][:].bitcast(F32), in_=q_ps[g][:].rearrange("w h i -> w (h i)"))

        def quantise_v(b, h):
            v_codes[b, h] = operand.tile([P, D], U32, name="v_codes_%d_%d" % (b, h), align_bytes=64)
            v_scales[b, h] = operand.tile([P, D], U8, name="v_scales_%d_%d" % (b, h), align_bytes=64)
            nc.vector.quantize_mx(
                out=v_codes[b, h][:].bitcast(FP8X4),
                scales=v_scales[b, h][:],
                in_=v_grouped[b, h][:].rearrange("p d r -> p (d r)"),
            )

        def keep_warm():
            idle = psum.tile([P, P], F32, tag="scores", bufs=BANKS["scores"], name="idle")
            nc.tensor.matmul(idle[:], lhsT=ones[:], rhs=ones[:], start=True, stop=True)

        def distances(g):
            b, t = divmod(g, TILES)
            d_sq[g] = psum.tile([P, S], F32, tag="d_sq", bufs=BANKS["d_sq"], name="d_sq")
            queries = feat_t[b][:, TILES + t, :]
            keys = feat_t[b][:, 0:TILES, :].rearrange("f t p -> f (t p)")
            if g in VECTOR_GROUPS:
                nc.tensor.matmul(d_sq[g][:], lhsT=queries, rhs=keys, start=True, stop=True)
                return
            for c in range(TILES):
                columns = slice(c * P, (c + 1) * P)
                nc.tensor.matmul(d_sq[g][:, columns], lhsT=keys[:, columns], rhs=queries, start=True, stop=True)

        def radial(u):
            g, h = divmod(u, H)
            rbf[u] = work.tile([P, S], F32, name="rbf", bufs=10)
            nc.scalar.activation(
                out=rbf[u][:],
                in_=d_sq[g][:],
                func=FUNC.Exp,
                scale=two_beta[:, h : h + 1],
                bias=log_height[:, h : h + 1],
            )

        def first_matmul(u):
            g, h = divmod(u, H)
            q_heads = q_t[g][:].rearrange("w (h i c) -> w h i c", h=H, c=CHUNKS)
            for c in range(CHUNKS):
                nc.tensor.matmul(
                    scores[u][:],
                    lhsT=q_heads[:, h, :, c],
                    rhs=k_t[g // TILES, h][:, :, c],
                    start=(c == 0 and (u % 2 != BIAS_FIRST or g in VECTOR_GROUPS)),
                    stop=(c == CHUNKS - 1 and (u % 2 == BIAS_FIRST or g in VECTOR_GROUPS)),
                )

        def add_bias(u):
            if u // H in VECTOR_GROUPS:
                return
            for c in range(TILES):
                nc.tensor.matmul(
                    scores[u][:, c * P : (c + 1) * P],
                    lhsT=rbf[u][:, c * P : (c + 1) * P],
                    rhs=ident_f32[:],
                    is_transpose=True,
                    start=(u % 2 == BIAS_FIRST and c == 0),
                    stop=(u % 2 != BIAS_FIRST and c == TILES - 1),
                )

        def add_on_vector(u):
            if u // H in VECTOR_GROUPS:
                total[u] = work.tile([P, S], F32, name="total", bufs=3)
                nc.vector.tensor_add(out=total[u][:], in0=rbf[u][:], in1=scores[u][:])

        def logits(u):
            g, h = divmod(u, H)
            if h == 0:
                neg_max[g] = work.tile([P, H], F32, name="neg_max", bufs=3)
            minus_z[u] = work.tile([P, S], F32, name="minus_z", bufs=8)
            nc.vector.tensor_scalar(
                out=minus_z[u][:],
                in0=(total[u] if g in VECTOR_GROUPS else scores[u])[:],
                scalar1=minus_sign[:, h : h + 1],
                scalar2=None,
                op0=ALU.mult,
                op1=ALU.min,
                accum_out=neg_max[g][:, h : h + 1],
            )

        def exponent(u):
            g, h = divmod(u, H)
            if h == 0:
                e_bf[g] = work.tile([P, H * S], BF16, name="e_bf", bufs=3)
                row_sum[g] = work.tile([P, H], F32, name="row_sum", bufs=3)
            nc.scalar.activation(
                out=e_bf[g][:, h * S : (h + 1) * S].rearrange("i (u p e) -> i u p e", u=HALVES, e=HALVES),
                in_=minus_z[u][:].rearrange("i (u e p) -> i u p e", u=HALVES, e=HALVES),
                func=FUNC.Exp,
                scale=-1.0,
                bias=neg_max[g][:, h : h + 1],
                accum_out=row_sum[g][:, h : h + 1],
            )

        def turn_e(g, heads):
            e_words = e_bf[g][:].bitcast(F32)
            bank = "scores" if g == GROUPS - 1 else "turn"
            e_ps[g, heads] = psum.tile([P, PAIR, HALVES, P], F32, tag=bank, bufs=BANKS[bank], name="e_ps")
            for x, h in enumerate(heads):
                for u in range(HALVES):
                    first = (h * HALVES + u) * P
                    nc.tensor.transpose(e_ps[g, heads][:, x, u, :], e_words[:, first : first + P], ident_f32[:])

        def copy_e(g, heads, copy):
            e_grouped[g, heads] = work.tile([P, PAIR * P * PACK], BF16, name="e_grouped", bufs=4, align_bytes=64)
            copy(
                out=e_grouped[g, heads][:, 0 : len(heads) * P * PACK]
                .bitcast(F32)
                .rearrange("p (h i u) -> p h i u", h=len(heads), u=HALVES),
                in_=e_ps[g, heads][:, 0 : len(heads)].rearrange("p h u i -> p h i u"),
            )

        def quantise_e(g, heads):
            e_codes[g, heads] = work.tile([P, PAIR * P], U32, name="e_codes", bufs=3, align_bytes=64)
            e_scales[g, heads] = work.tile([P, PAIR * P], U8, name="e_scales", bufs=3, align_bytes=64)
            used = len(heads) * P
            nc.vector.quantize_mx(
                out=e_codes[g, heads][:, 0:used].bitcast(FP8X4),
                scales=e_scales[g, heads][:, 0:used],
                in_=e_grouped[g, heads][:, 0 : used * PACK],
            )

        def reciprocal(g):
            inv_sum[g] = work.tile([P, H], F32, name="inv_sum", bufs=3)
            nc.vector.reciprocal(out=inv_sum[g][:], in_=row_sum[g][:])

        def second_matmul(g, heads):
            bank = "acc"
            if g == GROUPS - 1:
                bank = "turn" if H - 1 not in heads else "d_sq"
            acc[g, heads] = psum.tile([P, PAIR, D], F32, tag=bank, bufs=BANKS[bank], name="acc")
            for x, h in enumerate(heads):
                nc.tensor.matmul_mx(
                    out=acc[g, heads][:, x, :],
                    lhsT=e_codes[g, heads][:, x * P : (x + 1) * P].bitcast(FP8X4),
                    lhsT_scale=e_scales[g, heads][:, x * P : (x + 1) * P],
                    rhs=v_codes[g // TILES, h][:].bitcast(FP8X4),
                    rhs_scale=v_scales[g // TILES, h][:],
                    start=True,
                    stop=True,
                )

        def normalise(g, heads):
            b, t = divmod(g, TILES)
            result = work.tile([P, PAIR, D], F32, bufs=6)
            inv = inv_sum[g][:, heads[0] : heads[0] + len(heads)]
            if not normalised_by_scalar(g, heads):
                nc.vector.tensor_mul(
                    out=result[:, 0 : len(heads), :],
                    in0=acc[g, heads][:, 0 : len(heads), :],
                    in1=inv.unsqueeze(2).to_broadcast([P, len(heads), D]),
                )
            else:
                for x in range(len(heads)):
                    nc.scalar.activation(
                        out=result[:, x, :], in_=acc[g, heads][:, x, :], func=FUNC.Copy, scale=inv[:, x : x + 1]
                    )
            nc.sync.dma_start(
                out=out[b].rearrange("h (p t) d -> t p h d", t=TILES)[t, :, heads[0] : heads[0] + len(heads), :],
                in_=result[:, 0 : len(heads), :],
            )

        def logits_step(s):
            if AD and 0 <= s + LL + AD < UNITS:
                add_on_vector(s + LL + AD)
            if 0 <= s + LL < UNITS:
                if not AD:
                    add_on_vector(s + LL)
                logits(s + LL)

        for i in range(W1):
            keep_warm()
        turn_q(0)
        turn_features(0, 0)
        spread(slice(0, 4))
        turn_k(0, 0)
        copy_features(0, 0)
        copy_params(slice(0, 4))
        for i in range(W2):
            keep_warm()
        distances(0)
        turn_features(0, 1)
        copy_q(0, nc.vector.tensor_copy)
        copy_k(0, 0)
        copy_features(0, 1)
        for h in range(H):
            radial(h)

        for s in range(first_step + 1, last_step + 1):
            if not TL:
                for piece in pieces_due(s, TE):
                    turn_e(*piece)
            head = k_due(s)
            if head is not None:
                turn_k(head[0], head[1])
            g = q_due(s)
            if g is not None:
                turn_q(g)
            if s in FEATURES_DUE:
                turn_features(*FEATURES_DUE[s])
            if TL:
                for piece in pieces_due(s, TE):
                    turn_e(*piece)
            u = s + LEAD
            if 0 <= u < UNITS:
                scores[u] = psum.tile([P, S], F32, tag="scores", bufs=BANKS["scores"], name="scores")
                if u % 2 == BIAS_FIRST:
                    add_bias(u)
                    if MXE:
                        for piece in pieces_due(s, MX):
                            second_matmul(*piece)
                    first_matmul(u)
                else:
                    first_matmul(u)
                    add_bias(u)
            g = DIS1.get(s, due(s, DIS, H, GROUPS))
            if g is not None and (g > 1 or s in DIS1):
                distances(g)
            if not (MXE and 0 <= u < UNITS and u % 2 == BIAS_FIRST):
                for piece in pieces_due(s, MX):
                    second_matmul(*piece)

            if EXPFIRST and 0 <= s < UNITS:
                exponent(s)
            g = RAD1.get(s, due(s, RAD, H, GROUPS))
            if g is not None and (g > 1 or s in RAD1):
                for h in range(H):
                    radial(g * H + h)
            if not EXPFIRST and 0 <= s < UNITS:
                exponent(s)
            g = q_due(s - CQ)
            if g is not None and g > 0 and not q_on_vector(g):
                copy_q(g, nc.scalar.copy)
            for piece in pieces_due(s, CE):
                if copied_by_scalar(*piece):
                    copy_e(*piece, nc.scalar.copy)
            for piece in pieces_due(s, NO):
                if normalised_by_scalar(*piece):
                    normalise(*piece)

            head = k_due(s - CK)
            if head is not None and head != (0, 0) and KF:
                copy_k(head[0], head[1])
            if QF:
                for piece in pieces_due(s, QU):
                    quantise_e(*piece)
            if VO:
                logits_step(s)
            for piece in pieces_due(s, CE):
                if not copied_by_scalar(*piece):
                    copy_e(*piece, nc.vector.tensor_copy)
            if not VO:
                logits_step(s)
            if s - FS in FEATURES_DUE:
                copy_features(*FEATURES_DUE[s - FS])
            head = k_due(s - CK)
            if head is not None and head != (0, 0) and not KF:
                copy_k(head[0], head[1])
            g = q_due(s)
            if g is not None and g > 0 and q_on_vector(g):
                copy_q(g, nc.vector.tensor_copy)
            g = due(s, RE, H, GROUPS)
            if g is not None:
                reciprocal(g)
            if not QF:
                for piece in pieces_due(s, QU):
                    quantise_e(*piece)
            for piece in pieces_due(s, NO):
                if not normalised_by_scalar(*piece):
                    normalise(*piece)
            head = v_due(s - 7)
            if head is not None:
                quantise_v(head[0], head[1])
